import numpy as np
import ml_dtypes


def mxq(x, axis, fmt="e4m3"):
    dtype, down = {"e4m3": (ml_dtypes.float8_e4m3fn, 7), "e5m2": (ml_dtypes.float8_e5m2, 14)}[fmt]
    v = np.moveaxis(np.asarray(x, np.float32).astype(ml_dtypes.bfloat16).astype(np.float64), axis, -1)
    blocks = v.reshape(v.shape[:-1] + (-1, 32))
    amax = np.abs(blocks).max(-1, keepdims=True)
    byte = np.maximum(np.where(amax > 0, np.frexp(amax)[1] - 1 + 127, 0) - down, 1)
    scale = np.exp2(byte - 127.0)
    codes = (blocks / scale).astype(np.float32).astype(dtype).astype(np.float64)
    return np.moveaxis((codes * scale).reshape(v.shape), -1, axis)


WIDE = False


def mx_kscale(k):
    if not WIDE:
        return np.ones(k)
    levels = np.array([10, -10, 5, -5, 0])
    if k % 512:
        return np.exp2(np.random.permutation(np.resize(levels, k // 32))).repeat(32)
    a = np.empty((k // 512, 16))
    for p in range(k // 512):
        a[p, :8] = np.random.permutation(np.resize(levels, 8))
        for g in range(8):
            far = levels[np.abs(levels - a[p, g]) >= 10]
            a[p, g + 8] = far[np.random.randint(len(far))]
    return np.exp2(a.ravel()).repeat(32)


BF16 = ml_dtypes.bfloat16


def bf(x):
    return np.asarray(x, np.float32).astype(BF16)


def f64(x):
    return np.asarray(x).astype(np.float64)


N, S, K, Yd, Xd = 4096, 4, 16, 512, 256
LOG_2PI = np.log(2.0 * np.pi)


def softplus(v):
    return np.maximum(v, 0.0) + np.log(1.0 + np.exp(-np.abs(v)))


def log_softmax(v, axis):
    m = v - v.max(axis, keepdims=True)
    return m - np.log(np.exp(m).sum(axis, keepdims=True))


def mv_gaussian_log_prob(value, mu, sig_diags, event_shape):
    diff = value - mu
    M = np.sum((diff / sig_diags) ** 2, axis=-1)
    half_log_det = np.sum(np.log(sig_diags), axis=-1)
    return -0.5 * (event_shape * LOG_2PI + M) - half_log_det


def setup_inputs():
    s = mx_kscale(Yd)
    return {"Y": bf(np.random.standard_normal((N, Yd)) * 0.5 * s),
            "We_mu": bf(np.random.standard_normal((Yd, Xd)) * 2.0 / np.sqrt(Yd) / s[:, None]),
            "be_mu": bf(np.random.standard_normal(Xd) * 0.1),
            "We_sig": bf(np.random.standard_normal((Yd, Xd)) * 1.0 / np.sqrt(Yd) / s[:, None]),
            "be_sig": bf(-3.0 + np.random.standard_normal(Xd) * 0.1),
            "phi_mus": bf(np.random.standard_normal((K, Xd)) * 3.0 / np.sqrt(Xd)),
            "phi_sigs": bf(1.0 + (np.random.random_sample((K, Xd)) - 0.5) * 9.0 / np.sqrt(Xd)),
            "phi_logits": bf(np.random.standard_normal(K))}


def reference(Y, We_mu, be_mu, We_sig, be_sig, phi_mus, phi_sigs, phi_logits):
    Yq = mxq(f64(Y), 1, "e4m3")
    enc_mu = (Yq @ mxq(f64(We_mu), 0, "e4m3")) + f64(be_mu)
    enc_sig = softplus((Yq @ mxq(f64(We_sig), 0, "e4m3")) + f64(be_sig)) + 1e-3
    log_pi = log_softmax(f64(phi_logits), -1)
    std_k = enc_sig[:, None, :] + f64(phi_sigs)[None, :, :]
    z_logits = log_pi[None, :] + mv_gaussian_log_prob(enc_mu[:, None, :], f64(phi_mus)[None, :, :], std_k, Xd)
    z_log_probs = log_softmax(z_logits, -1)
    return enc_mu, enc_sig, z_log_probs

@@ -1,0 +1,405 @@
+from contextlib import ExitStack
+
+import concourse.mybir as mybir
+from concourse.masks import make_identity
+
+F32 = mybir.dt.float32
+BF16 = mybir.dt.bfloat16
+U32 = mybir.dt.uint32
+U8 = mybir.dt.uint8
+FP8X4 = mybir.dt.float8_e4m3fn_x4
+ALU = mybir.AluOpType
+ACT = mybir.ActivationFunctionType
+AX = mybir.AxisListType
+
+P = 128
+N_ROWS = 4096
+K_IN = 512
+D = 256
+H = D // P
+KC = 16
+CHUNK = 512
+TPC = CHUNK // P
+N_CHUNKS = N_ROWS // CHUNK
+N_TILES = N_ROWS // P
+N_UNITS = N_CHUNKS * KC
+PACK = 4
+
+SIG_FLOOR = 0.001
+SOFTPLUS_LINEAR_FROM = 40.0
+
+ROW_PHI_MUS = 0
+ROW_PHI_SIGS = KC
+ROW_BE_MU = 2 * KC
+ROW_BE_SIG = 2 * KC + 1
+
+GPSIMD_EVERY = 3
+SUM_LEAD = 3
+REDUCE_LAG = 3
+NEXT_CHUNK_AT = 10
+SCALAR_FROM = 4
+BIG_SLOTS = KC
+
+FLOPS = 2 * N_ROWS * K_IN * 2 * D
+
+
+def tile_deepgmm_pa_t_kernel(
+    tc, Y, We_mu, be_mu, We_sig, be_sig, phi_mus, phi_sigs, phi_logits, out_0, out_1, out_2
+):
+    nc = tc.nc
+    y_view = Y.rearrange("(p t) k -> p (t k)", t=N_TILES)
+    mu_view = out_0.rearrange("(p t) d -> p t d", t=N_TILES)
+    sig_view = out_1.rearrange("(p t) d -> p t d", t=N_TILES)
+    z_view = out_2.rearrange("(p t) k -> p (t k)", t=N_TILES)
+
+    with ExitStack() as ctx:
+        ctx.enter_context(tc.manual_schedule())
+        keep = ctx.enter_context(tc.tile_pool(name="keep", bufs=1))
+
+        ident = keep.tile([P, P], F32, name="ident")
+        w_codes = keep.tile([P, 2 * D], U32, name="w_codes", align_bytes=64)
+        w_scales = keep.tile([P, 2 * D], U8, name="w_scales", align_bytes=64)
+        y_codes = keep.tile([P, N_ROWS], U32, name="y_codes", align_bytes=64)
+        y_scales = keep.tile([P, N_ROWS], U8, name="y_scales", align_bytes=64)
+        par = keep.tile([P, H, P], F32, name="par")
+        mu_shift = keep.tile([P, H, KC], F32, name="mu_shift")
+        sig_shift = keep.tile([P, H, KC], F32, name="sig_shift")
+        be_mu_rows = keep.tile([P, D], F32, name="be_mu_rows")
+        logit_rows = keep.tile([P, KC], F32, name="logit_rows")
+        one = keep.tile([P, 1], F32, name="one")
+        half = keep.tile([P, 1], F32, name="half")
+        ln_half = keep.tile([P, 1], F32, name="ln_half")
+        half_ln_half = keep.tile([P, 1], F32, name="half_ln_half")
+        sig_t = keep.tile([P, N_CHUNKS, H, CHUNK], F32, name="sig_t")
+        energy = keep.tile([P, KC, N_TILES], F32, name="energy")
+
+        log_pool = ctx.enter_context(tc.tile_pool(name="logs", bufs=KC + 2))
+        sum_pool = ctx.enter_context(tc.tile_pool(name="log_sums", bufs=SUM_LEAD + 3))
+        big_pool = ctx.enter_context(tc.tile_pool(name="big", bufs=BIG_SLOTS))
+        out_pool = ctx.enter_context(tc.tile_pool(name="outs", bufs=3))
+        psum = ctx.enter_context(tc.psum_pool(name="psum", bufs=4))
+
+        def d_layout_sums(c, first_block):
+            rows = slice(c * CHUNK, (c + 1) * CHUNK)
+            sums = []
+            for h in range(H):
+                cols = slice((first_block + h) * P, (first_block + h + 1) * P)
+                d_sum = psum.tile([P, CHUNK], F32, name="d_sum", tag="d_sum")
+                nc.tensor.matmul_mx(
+                    out=d_sum[:],
+                    lhsT=w_codes[:, cols].bitcast(FP8X4),
+                    lhsT_scale=w_scales[:, cols],
+                    rhs=y_codes[:, rows].bitcast(FP8X4),
+                    rhs_scale=y_scales[:, rows],
+                    start=True,
+                    stop=True,
+                )
+                sums.append(d_sum)
+            return sums
+
+        make_identity(nc, ident[:])
+
+        rows_bf = keep.tile([P, D], BF16, name="rows_bf")
+        nc.vector.memset(rows_bf[:], 0.0)
+        nc.scalar.dma_start(out=rows_bf[ROW_PHI_MUS : ROW_PHI_MUS + KC, :], in_=phi_mus)
+        nc.scalar.dma_start(out=rows_bf[ROW_PHI_SIGS : ROW_PHI_SIGS + KC, :], in_=phi_sigs)
+        nc.scalar.dma_start(out=rows_bf[ROW_BE_MU : ROW_BE_MU + 1, :], in_=be_mu.rearrange("(o d) -> o d", o=1))
+        nc.scalar.dma_start(out=rows_bf[ROW_BE_SIG : ROW_BE_SIG + 1, :], in_=be_sig.rearrange("(o d) -> o d", o=1))
+        be_mu_bf = keep.tile([P, D], BF16, name="be_mu_bf")
+        nc.scalar.dma_start(out=be_mu_bf[:], in_=be_mu.partition_broadcast(P))
+        logit_bf = keep.tile([P, KC], BF16, name="logit_bf")
+        nc.scalar.dma_start(out=logit_bf[:], in_=phi_logits.partition_broadcast(P))
+        nc.vector.memset(one[:], 1.0)
+        nc.vector.memset(half[:], 0.5)
+
+        y_raw = []
+        w_raw = big_pool.tile([P, PACK, 2 * D], BF16, name="w_raw", tag="big", align_bytes=64)
+        for c in range(N_CHUNKS):
+            y_chunk = big_pool.tile([P, TPC * K_IN], BF16, name="y_chunk", tag="big", align_bytes=64)
+            nc.sync.dma_start(out=y_chunk[:], in_=y_view[:, c * TPC * K_IN : (c + 1) * TPC * K_IN])
+            y_raw.append(y_chunk)
+            if c == 0:
+                for m, weight in enumerate((We_mu, We_sig)):
+                    nc.sync.dma_start(
+                        out=w_raw[:, :, m * D : (m + 1) * D], in_=weight.rearrange("(q t) c -> q t c", t=PACK)
+                    )
+
+        y_banks = {}
+        y_grps = {}
+
+        def transpose_y(c):
+            words = y_raw[c][:].bitcast(F32)
+            y_banks[c] = []
+            for pair in range(TPC // 2):
+                y_t = psum.tile([P, 2, 2 * P], F32, name="y_t", tag="acc")
+                for i in range(2):
+                    first_word = (2 * pair + i) * (K_IN // 2)
+                    for u in range(2):
+                        nc.tensor.transpose(
+                            y_t[:, u, i * P : (i + 1) * P],
+                            words[:, first_word + u : first_word + K_IN // 2 : 2],
+                            ident[:],
+                        )
+                y_banks[c].append(y_t)
+
+        def regroup_y(c):
+            y_grp = big_pool.tile([P, PACK * CHUNK], BF16, name="y_grp", tag="big", align_bytes=64)
+            grp_words = y_grp[:].bitcast(F32)
+            for pair in range(TPC // 2):
+                nc.vector.tensor_copy(
+                    out=grp_words[:, pair * 4 * P : (pair + 1) * 4 * P].rearrange("p (n u) -> p n u", u=2),
+                    in_=y_banks[c][pair][:].rearrange("p u n -> p n u"),
+                )
+            y_grps[c] = y_grp
+
+        transpose_y(0)
+        regroup_y(0)
+
+        w_grp = big_pool.tile([P, 2 * D, PACK], BF16, name="w_grp", tag="big", align_bytes=64)
+        nc.vector.tensor_copy(out=w_grp[:], in_=w_raw[:].rearrange("p t c -> p c t"))
+        rows_f32 = keep.tile([P, D], F32, name="rows_f32")
+        nc.vector.tensor_copy(out=rows_f32[:], in_=rows_bf[:])
+        nc.vector.quantize_mx(
+            out=w_codes[:].bitcast(FP8X4), scales=w_scales[:], in_=w_grp[:].rearrange("p c t -> p (c t)")
+        )
+        par_ps = psum.tile([P, H, P], F32, name="par_ps", tag="acc")
+        for h in range(H):
+            nc.tensor.transpose(par_ps[:, h, :], rows_f32[:, h * P : (h + 1) * P], ident[:])
+        nc.vector.tensor_copy(out=par[:], in_=par_ps[:])
+        nc.vector.tensor_copy(out=be_mu_rows[:], in_=be_mu_bf[:])
+        nc.vector.tensor_copy(out=logit_rows[:], in_=logit_bf[:])
+        for h in range(H):
+            nc.vector.tensor_scalar(
+                out=mu_shift[:, h, :],
+                in0=par[:, h, ROW_PHI_MUS : ROW_PHI_MUS + KC],
+                scalar1=par[:, h, ROW_BE_MU : ROW_BE_MU + 1],
+                scalar2=None,
+                op0=ALU.subtract,
+            )
+        nc.vector.tensor_scalar(
+            out=sig_shift[:],
+            in0=par[:, :, ROW_PHI_SIGS : ROW_PHI_SIGS + KC],
+            scalar1=SIG_FLOOR,
+            scalar2=None,
+            op0=ALU.add,
+        )
+
+        def prepare(c):
+            if c + 1 < N_CHUNKS:
+                transpose_y(c + 1)
+            rows = slice(c * CHUNK, (c + 1) * CHUNK)
+            nc.vector.quantize_mx(out=y_codes[:, rows].bitcast(FP8X4), scales=y_scales[:, rows], in_=y_grps[c][:])
+            sig_sums = d_layout_sums(c, H)
+            mu_banks = []
+            for pair in range(TPC // 2):
+                mu_n = psum.tile([P, 2, D], F32, name="mu_n", tag="acc")
+                for i in range(2):
+                    cols = slice(c * CHUNK + (2 * pair + i) * P, c * CHUNK + (2 * pair + i + 1) * P)
+                    nc.tensor.matmul_mx(
+                        out=mu_n[:, i, :],
+                        lhsT=y_codes[:, cols].bitcast(FP8X4),
+                        lhsT_scale=y_scales[:, cols],
+                        rhs=w_codes[:, 0:D].bitcast(FP8X4),
+                        rhs_scale=w_scales[:, 0:D],
+                        start=True,
+                        stop=True,
+                    )
+                mu_banks.append(mu_n)
+            if c + 1 < N_CHUNKS:
+                regroup_y(c + 1)
+            for h in range(H):
+                nc.vector.tensor_scalar(
+                    out=sig_t[:, c, h, :],
+                    in0=sig_sums[h][:],
+                    scalar1=par[:, h, ROW_BE_SIG : ROW_BE_SIG + 1],
+                    scalar2=SOFTPLUS_LINEAR_FROM,
+                    op0=ALU.add,
+                    op1=ALU.min,
+                )
+            mu_out = out_pool.tile([P, TPC, D], F32, name="mu_out", tag="rows_out")
+            for pair in range(TPC // 2):
+                nc.vector.tensor_tensor(
+                    out=mu_out[:, 2 * pair : 2 * pair + 2, :],
+                    in0=mu_banks[pair][:],
+                    in1=be_mu_rows[:].unsqueeze(1).to_broadcast([P, 2, D]),
+                    op=ALU.add,
+                )
+            nc.sync.dma_start(out=mu_view[:, c * TPC : (c + 1) * TPC, :], in_=mu_out[:])
+
+        def softplus_exp(c):
+            nc.scalar.activation(out=sig_t[:, c, :, :], in_=sig_t[:, c, :, :], func=ACT.Exp)
+
+        def softplus_log(c):
+            nc.scalar.activation(out=sig_t[:, c, :, :], in_=sig_t[:, c, :, :], func=ACT.Ln, bias=one[:])
+
+        def softplus_max(c):
+            sig_sums = d_layout_sums(c, H)
+            for h in range(H):
+                nc.vector.scalar_tensor_tensor(
+                    out=sig_t[:, c, h, :],
+                    in0=sig_sums[h][:],
+                    scalar=par[:, h, ROW_BE_SIG : ROW_BE_SIG + 1],
+                    in1=sig_t[:, c, h, :],
+                    op0=ALU.add,
+                    op1=ALU.max,
+                )
+
+        def store_enc_sig(c):
+            sig_out = out_pool.tile([P, TPC, D], F32, name="sig_out", tag="rows_out")
+            for pair in range(TPC // 2):
+                sig_n = psum.tile([P, 2, D], F32, name="sig_n", tag="acc")
+                for i in range(2):
+                    cols = slice((2 * pair + i) * P, (2 * pair + i + 1) * P)
+                    for h in range(H):
+                        nc.tensor.transpose(sig_n[:, i, h * P : (h + 1) * P], sig_t[:, c, h, cols], ident[:])
+                nc.vector.tensor_scalar(
+                    out=sig_out[:, 2 * pair : 2 * pair + 2, :],
+                    in0=sig_n[:],
+                    scalar1=SIG_FLOOR,
+                    scalar2=None,
+                    op0=ALU.add,
+                )
+            nc.sync.dma_start(out=sig_view[:, c * TPC : (c + 1) * TPC, :], in_=sig_out[:])
+
+        logs = {}
+        wgts = {}
+        log_sums = {}
+        accs = {}
+        mu_sums = {}
+
+        def squarer(j):
+            if j % GPSIMD_EVERY == GPSIMD_EVERY - 1:
+                return "gpsimd"
+            if j >= N_UNITS - KC + SCALAR_FROM:
+                return "scalar"
+            return "vector"
+
+        def take_logs(c):
+            for k in range(KC):
+                unit_logs = log_pool.tile([P, H, CHUNK], F32, name="unit_logs")
+                for h in range(H):
+                    nc.scalar.activation(
+                        out=unit_logs[:, h, :], in_=sig_t[:, c, h, :], func=ACT.Ln, bias=sig_shift[:, h, k : k + 1]
+                    )
+                logs[c * KC + k] = unit_logs
+
+        def take_weights(c):
+            for j in range(c * KC, (c + 1) * KC):
+                wgt = big_pool.tile([P, H, CHUNK], F32, name="wgt", tag="big", align_bytes=64)
+                if squarer(j) == "vector":
+                    nc.scalar.activation(out=wgt[:], in_=logs[j][:], func=ACT.Exp, bias=ln_half[:], scale=-2.0)
+                else:
+                    nc.scalar.activation(out=wgt[:], in_=logs[j][:], func=ACT.Exp, bias=half_ln_half[:], scale=-1.0)
+                wgts[j] = wgt
+
+        def add_logs(j):
+            log_sum = sum_pool.tile([P, CHUNK], F32, name="log_sum")
+            nc.gpsimd.tensor_tensor(out=log_sum[:], in0=logs[j][:, 0, :], in1=logs[j][:, 1, :], op=ALU.add)
+            log_sums[j] = log_sum
+
+        def weighted_squares(j):
+            c, k = divmod(j, KC)
+            wgt = wgts[j]
+            for step in range(2 if squarer(j) == "vector" else 1):
+                for h in range(H):
+                    nc.vector.scalar_tensor_tensor(
+                        out=wgt[:, h, :],
+                        in0=mu_sums[c][h][:],
+                        scalar=mu_shift[:, h, k : k + 1],
+                        in1=wgt[:, h, :],
+                        op0=ALU.subtract,
+                        op1=ALU.mult,
+                    )
+            if squarer(j) == "gpsimd":
+                nc.gpsimd.tensor_tensor(out=wgt[:], in0=wgt[:], in1=wgt[:], op=ALU.mult)
+            if squarer(j) == "scalar":
+                nc.scalar.activation(out=wgt[:], in_=wgt[:], func=ACT.Square)
+
+        def add_over_halves(j):
+            acc = psum.tile([P, TPC, P], F32, name="acc", tag="acc")
+            for t in range(TPC):
+                cols = slice(t * P, (t + 1) * P)
+                parts = (log_sums[j][:, cols], wgts[j][:, 0, cols], wgts[j][:, 1, cols])
+                for i, part in enumerate(parts):
+                    nc.tensor.matmul(
+                        out=acc[:, t, :],
+                        lhsT=part,
+                        rhs=ident[:],
+                        is_transpose=True,
+                        start=(i == 0),
+                        stop=(i == len(parts) - 1),
+                    )
+            accs[j] = acc
+
+        def reduce_units(first, end):
+            for j in range(first, end):
+                c, k = divmod(j, KC)
+                nc.vector.tensor_reduce(
+                    out=energy[:, k, c * TPC : (c + 1) * TPC], in_=accs[j][:], axis=AX.X, op=ALU.add
+                )
+
+        prepare(0)
+        softplus_exp(0)
+        softplus_log(0)
+        nc.scalar.activation(out=ln_half[:], in_=half[:], func=ACT.Ln)
+        prepare(1)
+        softplus_max(0)
+        take_logs(0)
+        for c in range(2, N_CHUNKS):
+            prepare(c)
+        store_enc_sig(0)
+        nc.vector.tensor_scalar(out=half_ln_half[:], in0=ln_half[:], scalar1=0.5, scalar2=None, op0=ALU.mult)
+        mu_sums[0] = d_layout_sums(0, 0)
+        take_weights(0)
+        for c in range(1, N_CHUNKS):
+            softplus_exp(c)
+        for j in range(SUM_LEAD):
+            add_logs(j)
+
+        reduced = 0
+        for c in range(N_CHUNKS):
+            for j in range(c * KC, (c + 1) * KC):
+                if j == c * KC + NEXT_CHUNK_AT and c + 1 < N_CHUNKS:
+                    if c == 0:
+                        reduce_units(reduced, j)
+                        reduced = j
+                        for b in range(1, N_CHUNKS + 1):
+                            if b < N_CHUNKS:
+                                softplus_log(b)
+                                softplus_max(b)
+                            if b > 1:
+                                store_enc_sig(b - 1)
+                    mu_sums[c + 1] = d_layout_sums(c + 1, 0)
+                    take_logs(c + 1)
+                if j + SUM_LEAD < N_UNITS:
+                    add_logs(j + SUM_LEAD)
+                weighted_squares(j)
+                add_over_halves(j)
+                if j - REDUCE_LAG >= reduced:
+                    reduce_units(reduced, j - REDUCE_LAG + 1)
+                    reduced = j - REDUCE_LAG + 1
+            if c + 1 < N_CHUNKS:
+                take_weights(c + 1)
+        reduce_units(reduced, N_UNITS)
+
+        z = keep.tile([P, N_TILES, KC], F32, name="z")
+        z_max = keep.tile([P, N_TILES], F32, name="z_max")
+        z_exp = keep.tile([P, N_TILES, KC], F32, name="z_exp")
+        z_sum = keep.tile([P, N_TILES], F32, name="z_sum")
+        nc.vector.tensor_tensor(
+            out=z[:],
+            in0=logit_rows[:].unsqueeze(1).to_broadcast([P, N_TILES, KC]),
+            in1=energy[:].rearrange("p k t -> p t k"),
+            op=ALU.subtract,
+        )
+        nc.vector.tensor_reduce(out=z_max[:], in_=z[:], axis=AX.X, op=ALU.max)
+        nc.vector.tensor_tensor(
+            out=z[:], in0=z[:], in1=z_max[:].unsqueeze(2).to_broadcast([P, N_TILES, KC]), op=ALU.subtract
+        )
+        nc.scalar.activation(out=z_exp[:], in_=z[:], func=ACT.Exp)
+        nc.vector.tensor_reduce(out=z_sum[:], in_=z_exp[:], axis=AX.X, op=ALU.add)
+        nc.scalar.activation(out=z_sum[:], in_=z_sum[:], func=ACT.Ln)
+        nc.vector.tensor_tensor(
+            out=z[:], in0=z[:], in1=z_sum[:].unsqueeze(2).to_broadcast([P, N_TILES, KC]), op=ALU.subtract
+        )
+        nc.sync.dma_start(out=z_view, in_=z[:].rearrange("p t k -> p (t k)"))

@@ -33,11 +33,11 @@ ROW_PHI_SIGS = KC
 ROW_BE_MU = 2 * KC
 ROW_BE_SIG = 2 * KC + 1
 
-GPSIMD_EVERY = 3
-SUM_LEAD = 3
+VECTOR_EVERY = 8
 REDUCE_LAG = 3
 NEXT_CHUNK_AT = 10
-SCALAR_FROM = 4
+SCALAR_FROM = 2
+LOG_SLOTS = 24
 BIG_SLOTS = KC
 
 FLOPS = 2 * N_ROWS * K_IN * 2 * D
@@ -73,10 +73,9 @@ def tile_deepgmm_pa_t_kernel(
         sig_t = keep.tile([P, N_CHUNKS, H, CHUNK], F32, name="sig_t")
         energy = keep.tile([P, KC, N_TILES], F32, name="energy")
 
-        log_pool = ctx.enter_context(tc.tile_pool(name="logs", bufs=KC + 2))
-        sum_pool = ctx.enter_context(tc.tile_pool(name="log_sums", bufs=SUM_LEAD + 3))
+        log_pool = ctx.enter_context(tc.tile_pool(name="logs", bufs=LOG_SLOTS))
         big_pool = ctx.enter_context(tc.tile_pool(name="big", bufs=BIG_SLOTS))
-        out_pool = ctx.enter_context(tc.tile_pool(name="outs", bufs=3))
+        out_pool = ctx.enter_context(tc.tile_pool(name="outs", bufs=2))
         psum = ctx.enter_context(tc.psum_pool(name="psum", bufs=4))
 
         def d_layout_sums(c, first_block):
@@ -263,16 +262,15 @@ def tile_deepgmm_pa_t_kernel(
 
         logs = {}
         wgts = {}
-        log_sums = {}
         accs = {}
         mu_sums = {}
 
         def squarer(j):
-            if j % GPSIMD_EVERY == GPSIMD_EVERY - 1:
-                return "gpsimd"
-            if j >= N_UNITS - KC + SCALAR_FROM:
+            if j >= N_UNITS - KC + SCALAR_FROM and j % 2 == 1:
                 return "scalar"
-            return "vector"
+            if j % VECTOR_EVERY == VECTOR_EVERY - 1:
+                return "vector"
+            return "gpsimd"
 
         def take_logs(c):
             for k in range(KC):
@@ -291,11 +289,6 @@ def tile_deepgmm_pa_t_kernel(
                 else:
                     nc.scalar.activation(out=wgt[:], in_=logs[j][:], func=ACT.Exp, bias=half_ln_half[:], scale=-1.0)
                 wgts[j] = wgt
-
-        def add_logs(j):
-            log_sum = sum_pool.tile([P, CHUNK], F32, name="log_sum")
-            nc.gpsimd.tensor_tensor(out=log_sum[:], in0=logs[j][:, 0, :], in1=logs[j][:, 1, :], op=ALU.add)
-            log_sums[j] = log_sum
 
         def weighted_squares(j):
             c, k = divmod(j, KC)
@@ -319,7 +312,7 @@ def tile_deepgmm_pa_t_kernel(
             acc = psum.tile([P, TPC, P], F32, name="acc", tag="acc")
             for t in range(TPC):
                 cols = slice(t * P, (t + 1) * P)
-                parts = (log_sums[j][:, cols], wgts[j][:, 0, cols], wgts[j][:, 1, cols])
+                parts = (logs[j][:, 0, cols], logs[j][:, 1, cols], wgts[j][:, 0, cols], wgts[j][:, 1, cols])
                 for i, part in enumerate(parts):
                     nc.tensor.matmul(
                         out=acc[:, t, :],
@@ -353,8 +346,6 @@ def tile_deepgmm_pa_t_kernel(
         take_weights(0)
         for c in range(1, N_CHUNKS):
             softplus_exp(c)
-        for j in range(SUM_LEAD):
-            add_logs(j)
 
         reduced = 0
         for c in range(N_CHUNKS):
@@ -371,8 +362,6 @@ def tile_deepgmm_pa_t_kernel(
                                 store_enc_sig(b - 1)
                     mu_sums[c + 1] = d_layout_sums(c + 1, 0)
                     take_logs(c + 1)
-                if j + SUM_LEAD < N_UNITS:
-                    add_logs(j + SUM_LEAD)
                 weighted_squares(j)
                 add_over_halves(j)
                 if j - REDUCE_LAG >= reduced:

@@ -33,12 +33,19 @@ ROW_PHI_SIGS = KC
 ROW_BE_MU = 2 * KC
 ROW_BE_SIG = 2 * KC + 1
 
-VECTOR_EVERY = 8
-REDUCE_LAG = 3
-NEXT_CHUNK_AT = 10
-SCALAR_FROM = 2
-LOG_SLOTS = 24
-BIG_SLOTS = KC
+ENDS = (16, 38, 60, 82, 104, 120, 128)
+PARS = (1, 10, 1, 1)
+PAIRED = (4, 12)
+PAIRED_FIRST = (4, 8, 12)
+PAIRED_END = 112
+SCALAR_FROM = 0
+SUM_LAG = 3
+REDUCE_LAG = 5
+BIG_SLOTS = 32
+SIG_OUT_SLOTS = 3
+PAIR_SLOTS = 3
+SMALL_SLOTS = 8
+STAGE_SLOTS = 3
 
 FLOPS = 2 * N_ROWS * K_IN * 2 * D
 
@@ -59,8 +66,6 @@ def tile_deepgmm_pa_t_kernel(
         ident = keep.tile([P, P], F32, name="ident")
         w_codes = keep.tile([P, 2 * D], U32, name="w_codes", align_bytes=64)
         w_scales = keep.tile([P, 2 * D], U8, name="w_scales", align_bytes=64)
-        y_codes = keep.tile([P, N_ROWS], U32, name="y_codes", align_bytes=64)
-        y_scales = keep.tile([P, N_ROWS], U8, name="y_scales", align_bytes=64)
         par = keep.tile([P, H, P], F32, name="par")
         mu_shift = keep.tile([P, H, KC], F32, name="mu_shift")
         sig_shift = keep.tile([P, H, KC], F32, name="sig_shift")
@@ -70,26 +75,35 @@ def tile_deepgmm_pa_t_kernel(
         half = keep.tile([P, 1], F32, name="half")
         ln_half = keep.tile([P, 1], F32, name="ln_half")
         half_ln_half = keep.tile([P, 1], F32, name="half_ln_half")
-        sig_t = keep.tile([P, N_CHUNKS, H, CHUNK], F32, name="sig_t")
         energy = keep.tile([P, KC, N_TILES], F32, name="energy")
 
-        log_pool = ctx.enter_context(tc.tile_pool(name="logs", bufs=LOG_SLOTS))
         big_pool = ctx.enter_context(tc.tile_pool(name="big", bufs=BIG_SLOTS))
+        y_pool = ctx.enter_context(tc.tile_pool(name="ys", bufs=3))
+        stage_pool = ctx.enter_context(tc.tile_pool(name="stages", bufs=STAGE_SLOTS))
         out_pool = ctx.enter_context(tc.tile_pool(name="outs", bufs=2))
-        psum = ctx.enter_context(tc.psum_pool(name="psum", bufs=4))
+        mu_psum = ctx.enter_context(tc.psum_pool(name="mu_psum", bufs=3))
+        stage_psum = ctx.enter_context(tc.psum_pool(name="stage_psum", bufs=2))
+        acc_psum = ctx.enter_context(tc.psum_pool(name="acc_psum", bufs=3))
 
-        def d_layout_sums(c, first_block):
-            rows = slice(c * CHUNK, (c + 1) * CHUNK)
+        sig_out_pool = ctx.enter_context(tc.tile_pool(name="sig_outs", bufs=SIG_OUT_SLOTS))
+        pair_pool = ctx.enter_context(tc.tile_pool(name="pairs", bufs=PAIR_SLOTS))
+        small_pool = ctx.enter_context(tc.tile_pool(name="smalls", bufs=SMALL_SLOTS))
+        sig_outs = {}
+        codes = {}
+        scales = {}
+        sig = {}
+
+        def d_layout_sums(c, first_block, pool):
             sums = []
             for h in range(H):
                 cols = slice((first_block + h) * P, (first_block + h + 1) * P)
-                d_sum = psum.tile([P, CHUNK], F32, name="d_sum", tag="d_sum")
+                d_sum = pool.tile([P, CHUNK], F32, name="d_sum", tag="bank")
                 nc.tensor.matmul_mx(
                     out=d_sum[:],
                     lhsT=w_codes[:, cols].bitcast(FP8X4),
                     lhsT_scale=w_scales[:, cols],
-                    rhs=y_codes[:, rows].bitcast(FP8X4),
-                    rhs_scale=y_scales[:, rows],
+                    rhs=codes[c][:].bitcast(FP8X4),
+                    rhs_scale=scales[c][:],
                     start=True,
                     stop=True,
                 )
@@ -100,37 +114,28 @@ def tile_deepgmm_pa_t_kernel(
 
         rows_bf = keep.tile([P, D], BF16, name="rows_bf")
         nc.vector.memset(rows_bf[:], 0.0)
+        nc.vector.memset(one[:], 1.0)
+        nc.vector.memset(half[:], 0.5)
         nc.scalar.dma_start(out=rows_bf[ROW_PHI_MUS : ROW_PHI_MUS + KC, :], in_=phi_mus)
         nc.scalar.dma_start(out=rows_bf[ROW_PHI_SIGS : ROW_PHI_SIGS + KC, :], in_=phi_sigs)
         nc.scalar.dma_start(out=rows_bf[ROW_BE_MU : ROW_BE_MU + 1, :], in_=be_mu.rearrange("(o d) -> o d", o=1))
         nc.scalar.dma_start(out=rows_bf[ROW_BE_SIG : ROW_BE_SIG + 1, :], in_=be_sig.rearrange("(o d) -> o d", o=1))
-        be_mu_bf = keep.tile([P, D], BF16, name="be_mu_bf")
-        nc.scalar.dma_start(out=be_mu_bf[:], in_=be_mu.partition_broadcast(P))
-        logit_bf = keep.tile([P, KC], BF16, name="logit_bf")
-        nc.scalar.dma_start(out=logit_bf[:], in_=phi_logits.partition_broadcast(P))
-        nc.vector.memset(one[:], 1.0)
-        nc.vector.memset(half[:], 0.5)
+        nc.scalar.activation(out=ln_half[:], in_=half[:], func=ACT.Exp)
 
-        y_raw = []
-        w_raw = big_pool.tile([P, PACK, 2 * D], BF16, name="w_raw", tag="big", align_bytes=64)
-        for c in range(N_CHUNKS):
-            y_chunk = big_pool.tile([P, TPC * K_IN], BF16, name="y_chunk", tag="big", align_bytes=64)
-            nc.sync.dma_start(out=y_chunk[:], in_=y_view[:, c * TPC * K_IN : (c + 1) * TPC * K_IN])
-            y_raw.append(y_chunk)
-            if c == 0:
-                for m, weight in enumerate((We_mu, We_sig)):
-                    nc.sync.dma_start(
-                        out=w_raw[:, :, m * D : (m + 1) * D], in_=weight.rearrange("(q t) c -> q t c", t=PACK)
-                    )
-
+        y_raw = {}
         y_banks = {}
         y_grps = {}
+
+        def load_y(c):
+            y_chunk = y_pool.tile([P, TPC * K_IN], BF16, name="y_chunk", tag="y", align_bytes=64)
+            nc.sync.dma_start(out=y_chunk[:], in_=y_view[:, c * TPC * K_IN : (c + 1) * TPC * K_IN])
+            y_raw[c] = y_chunk
 
         def transpose_y(c):
             words = y_raw[c][:].bitcast(F32)
             y_banks[c] = []
             for pair in range(TPC // 2):
-                y_t = psum.tile([P, 2, 2 * P], F32, name="y_t", tag="acc")
+                y_t = stage_psum.tile([P, 2, 2 * P], F32, name="y_t", tag="bank")
                 for i in range(2):
                     first_word = (2 * pair + i) * (K_IN // 2)
                     for u in range(2):
@@ -142,118 +147,141 @@ def tile_deepgmm_pa_t_kernel(
                 y_banks[c].append(y_t)
 
         def regroup_y(c):
-            y_grp = big_pool.tile([P, PACK * CHUNK], BF16, name="y_grp", tag="big", align_bytes=64)
+            y_grp = y_pool.tile([P, PACK * CHUNK], BF16, name="y_grp", tag="y", align_bytes=64)
             grp_words = y_grp[:].bitcast(F32)
             for pair in range(TPC // 2):
-                nc.vector.tensor_copy(
+                copy = nc.scalar.copy if c == 0 and pair == 1 else nc.vector.tensor_copy
+                copy(
                     out=grp_words[:, pair * 4 * P : (pair + 1) * 4 * P].rearrange("p (n u) -> p n u", u=2),
                     in_=y_banks[c][pair][:].rearrange("p u n -> p n u"),
                 )
             y_grps[c] = y_grp
 
+        def quantize_y(c):
+            codes[c] = stage_pool.tile([P, CHUNK], U32, name="y_codes", align_bytes=64)
+            scales[c] = stage_pool.tile([P, CHUNK], U8, name="y_scales", align_bytes=64)
+            nc.vector.quantize_mx(out=codes[c][:].bitcast(FP8X4), scales=scales[c][:], in_=y_grps[c][:])
+
+        load_y(0)
+        w_raw = {}
+        for m, weight in ((1, We_sig), (0, We_mu)):
+            w_raw[m] = small_pool.tile([P, PACK, D], BF16, name="w_raw", tag="small", align_bytes=64)
+            nc.sync.dma_start(out=w_raw[m][:], in_=weight.rearrange("(q t) c -> q t c", t=PACK))
+        load_y(1)
+        be_mu_bf = keep.tile([P, D], BF16, name="be_mu_bf")
+        nc.sync.dma_start(out=be_mu_bf[:], in_=be_mu.partition_broadcast(P))
+        logit_bf = keep.tile([P, KC], BF16, name="logit_bf")
+        nc.sync.dma_start(out=logit_bf[:], in_=phi_logits.partition_broadcast(P))
+        pair_bf = keep.tile([P, len(PAIRED_FIRST), D], BF16, name="pair_bf")
+        for i, k in enumerate(PAIRED_FIRST):
+            nc.sync.dma_start(out=pair_bf[:, i, :], in_=phi_sigs[k, :].partition_broadcast(P))
+
+        w_grps = {}
+
+        def regroup_w(m):
+            w_grps[m] = small_pool.tile([P, D, PACK], BF16, name="w_grp", tag="small", align_bytes=64)
+            nc.vector.tensor_copy(out=w_grps[m][:], in_=w_raw[m][:].rearrange("p t c -> p c t"))
+
+        def quantize_w(m):
+            nc.vector.quantize_mx(
+                out=w_codes[:, m * D : (m + 1) * D].bitcast(FP8X4),
+                scales=w_scales[:, m * D : (m + 1) * D],
+                in_=w_grps[m][:].rearrange("p c t -> p (c t)"),
+            )
+
         transpose_y(0)
         regroup_y(0)
-
-        w_grp = big_pool.tile([P, 2 * D, PACK], BF16, name="w_grp", tag="big", align_bytes=64)
-        nc.vector.tensor_copy(out=w_grp[:], in_=w_raw[:].rearrange("p t c -> p c t"))
+        regroup_w(1)
         rows_f32 = keep.tile([P, D], F32, name="rows_f32")
         nc.vector.tensor_copy(out=rows_f32[:], in_=rows_bf[:])
-        nc.vector.quantize_mx(
-            out=w_codes[:].bitcast(FP8X4), scales=w_scales[:], in_=w_grp[:].rearrange("p c t -> p (c t)")
-        )
-        par_ps = psum.tile([P, H, P], F32, name="par_ps", tag="acc")
+        quantize_w(1)
+        par_ps = stage_psum.tile([P, H, P], F32, name="par_ps", tag="bank")
         for h in range(H):
             nc.tensor.transpose(par_ps[:, h, :], rows_f32[:, h * P : (h + 1) * P], ident[:])
+        quantize_y(0)
         nc.vector.tensor_copy(out=par[:], in_=par_ps[:])
-        nc.vector.tensor_copy(out=be_mu_rows[:], in_=be_mu_bf[:])
-        nc.vector.tensor_copy(out=logit_rows[:], in_=logit_bf[:])
-        for h in range(H):
-            nc.vector.tensor_scalar(
-                out=mu_shift[:, h, :],
-                in0=par[:, h, ROW_PHI_MUS : ROW_PHI_MUS + KC],
-                scalar1=par[:, h, ROW_BE_MU : ROW_BE_MU + 1],
-                scalar2=None,
-                op0=ALU.subtract,
-            )
-        nc.vector.tensor_scalar(
-            out=sig_shift[:],
-            in0=par[:, :, ROW_PHI_SIGS : ROW_PHI_SIGS + KC],
-            scalar1=SIG_FLOOR,
-            scalar2=None,
-            op0=ALU.add,
-        )
 
-        def prepare(c):
-            if c + 1 < N_CHUNKS:
-                transpose_y(c + 1)
-            rows = slice(c * CHUNK, (c + 1) * CHUNK)
-            nc.vector.quantize_mx(out=y_codes[:, rows].bitcast(FP8X4), scales=y_scales[:, rows], in_=y_grps[c][:])
-            sig_sums = d_layout_sums(c, H)
-            mu_banks = []
-            for pair in range(TPC // 2):
-                mu_n = psum.tile([P, 2, D], F32, name="mu_n", tag="acc")
-                for i in range(2):
-                    cols = slice(c * CHUNK + (2 * pair + i) * P, c * CHUNK + (2 * pair + i + 1) * P)
-                    nc.tensor.matmul_mx(
-                        out=mu_n[:, i, :],
-                        lhsT=y_codes[:, cols].bitcast(FP8X4),
-                        lhsT_scale=y_scales[:, cols],
-                        rhs=w_codes[:, 0:D].bitcast(FP8X4),
-                        rhs_scale=w_scales[:, 0:D],
-                        start=True,
-                        stop=True,
-                    )
-                mu_banks.append(mu_n)
-            if c + 1 < N_CHUNKS:
-                regroup_y(c + 1)
+        banks = {}
+
+        def sig_sums(c):
+            banks[c] = d_layout_sums(c, H, stage_psum)
+
+        def sig_clamp(c):
+            sig[c] = stage_pool.tile([P, H, CHUNK], F32, name="sig_t")
             for h in range(H):
                 nc.vector.tensor_scalar(
-                    out=sig_t[:, c, h, :],
-                    in0=sig_sums[h][:],
+                    out=sig[c][:, h, :],
+                    in0=banks[c][h][:],
                     scalar1=par[:, h, ROW_BE_SIG : ROW_BE_SIG + 1],
                     scalar2=SOFTPLUS_LINEAR_FROM,
                     op0=ALU.add,
                     op1=ALU.min,
                 )
+
+        def mu_rows(c):
+            banks[c] = []
+            for pair in range(TPC // 2):
+                mu_n = stage_psum.tile([P, 2, D], F32, name="mu_n", tag="bank")
+                for i in range(2):
+                    cols = slice((2 * pair + i) * P, (2 * pair + i + 1) * P)
+                    nc.tensor.matmul_mx(
+                        out=mu_n[:, i, :],
+                        lhsT=codes[c][:, cols].bitcast(FP8X4),
+                        lhsT_scale=scales[c][:, cols],
+                        rhs=w_codes[:, 0:D].bitcast(FP8X4),
+                        rhs_scale=w_scales[:, 0:D],
+                        start=True,
+                        stop=True,
+                    )
+                banks[c].append(mu_n)
+
+        def store_enc_mu(c):
             mu_out = out_pool.tile([P, TPC, D], F32, name="mu_out", tag="rows_out")
             for pair in range(TPC // 2):
                 nc.vector.tensor_tensor(
                     out=mu_out[:, 2 * pair : 2 * pair + 2, :],
-                    in0=mu_banks[pair][:],
+                    in0=banks[c][pair][:],
                     in1=be_mu_rows[:].unsqueeze(1).to_broadcast([P, 2, D]),
                     op=ALU.add,
                 )
             nc.sync.dma_start(out=mu_view[:, c * TPC : (c + 1) * TPC, :], in_=mu_out[:])
 
         def softplus_exp(c):
-            nc.scalar.activation(out=sig_t[:, c, :, :], in_=sig_t[:, c, :, :], func=ACT.Exp)
+            for h in range(H):
+                nc.scalar.activation(out=sig[c][:, h, :], in_=sig[c][:, h, :], func=ACT.Exp)
 
         def softplus_log(c):
-            nc.scalar.activation(out=sig_t[:, c, :, :], in_=sig_t[:, c, :, :], func=ACT.Ln, bias=one[:])
+            for h in range(H):
+                nc.scalar.activation(out=sig[c][:, h, :], in_=sig[c][:, h, :], func=ACT.Ln, bias=one[:])
 
         def softplus_max(c):
-            sig_sums = d_layout_sums(c, H)
             for h in range(H):
                 nc.vector.scalar_tensor_tensor(
-                    out=sig_t[:, c, h, :],
-                    in0=sig_sums[h][:],
+                    out=sig[c][:, h, :],
+                    in0=banks[c][h][:],
                     scalar=par[:, h, ROW_BE_SIG : ROW_BE_SIG + 1],
-                    in1=sig_t[:, c, h, :],
+                    in1=sig[c][:, h, :],
                     op0=ALU.add,
                     op1=ALU.max,
                 )
 
-        def store_enc_sig(c):
-            sig_out = out_pool.tile([P, TPC, D], F32, name="sig_out", tag="rows_out")
+        def sig_rows(c):
+            banks[c] = []
             for pair in range(TPC // 2):
-                sig_n = psum.tile([P, 2, D], F32, name="sig_n", tag="acc")
+                sig_n = stage_psum.tile([P, 2, D], F32, name="sig_n", tag="bank")
                 for i in range(2):
                     cols = slice((2 * pair + i) * P, (2 * pair + i + 1) * P)
                     for h in range(H):
-                        nc.tensor.transpose(sig_n[:, i, h * P : (h + 1) * P], sig_t[:, c, h, cols], ident[:])
+                        nc.tensor.transpose(sig_n[:, i, h * P : (h + 1) * P], sig[c][:, h, cols], ident[:])
+                banks[c].append(sig_n)
+
+        def store_enc_sig(c):
+            sig_out = sig_out_pool.tile([P, TPC, D], F32, name="sig_out")
+            sig_outs[c] = sig_out
+            for pair in range(TPC // 2):
                 nc.vector.tensor_scalar(
                     out=sig_out[:, 2 * pair : 2 * pair + 2, :],
-                    in0=sig_n[:],
+                    in0=banks[c][pair][:],
                     scalar1=SIG_FLOOR,
                     scalar2=None,
                     op0=ALU.add,
@@ -268,51 +296,107 @@ def tile_deepgmm_pa_t_kernel(
         def squarer(j):
             if j >= N_UNITS - KC + SCALAR_FROM and j % 2 == 1:
                 return "scalar"
-            if j % VECTOR_EVERY == VECTOR_EVERY - 1:
-                return "vector"
             return "gpsimd"
 
-        def take_logs(c):
-            for k in range(KC):
-                unit_logs = log_pool.tile([P, H, CHUNK], F32, name="unit_logs")
+        def is_paired(j):
+            return j % KC in (PAIRED_FIRST if j < KC else PAIRED) and j < PAIRED_END and j not in ENDS
+
+        stds = {}
+
+        def std_banks(j, halves):
+            c, k = divmod(j, KC)
+            stds[j] = {}
+            for h in halves:
+                std = stage_psum.tile([P, TPC, P], F32, name="std", tag="bank")
+                for t in range(TPC):
+                    parts = (
+                        sig_outs[c][:, t, h * P : (h + 1) * P],
+                        pair_rows[:, PAIRED_FIRST.index(k), h * P : (h + 1) * P],
+                    )
+                    for i, part in enumerate(parts):
+                        nc.tensor.matmul(
+                            out=std[:, t, :],
+                            lhsT=part,
+                            rhs=ident[:],
+                            is_transpose=True,
+                            start=(i == 0),
+                            stop=(i == len(parts) - 1),
+                        )
+                stds[j][h] = std
+
+        def multiply_pair(j):
+            c, k = divmod(j, KC)
+            product = small_pool.tile([P, CHUNK], F32, name="product", tag="small", align_bytes=64)
+            nc.vector.scalar_tensor_tensor(
+                out=product[:],
+                in0=sig[c][:, 0, :],
+                scalar=sig_shift[:, 0, k : k + 1],
+                in1=stds[j][1][:].rearrange("p t n -> p (t n)"),
+                op0=ALU.add,
+                op1=ALU.mult,
+            )
+            logs[j] = product
+
+        def divide_pair(j):
+            wgt = pair_pool.tile([P, H, CHUNK], F32, name="pair_wgt")
+            for h in range(H):
+                nc.vector.tensor_tensor(
+                    out=wgt[:, h, :],
+                    in0=stds[j][1 - h][:].rearrange("p t n -> p (t n)"),
+                    in1=wgts[j][:],
+                    op=ALU.mult,
+                )
+            wgts[j] = wgt
+
+        def take_logs(units, paired):
+            for j in units:
+                c, k = divmod(j, KC)
+                if is_paired(j) != paired:
+                    continue
+                if paired:
+                    nc.scalar.activation(out=logs[j][:], in_=logs[j][:], func=ACT.Ln)
+                    continue
+                unit_logs = big_pool.tile([P, H, CHUNK], F32, name="unit_logs", tag="big", align_bytes=64)
                 for h in range(H):
                     nc.scalar.activation(
-                        out=unit_logs[:, h, :], in_=sig_t[:, c, h, :], func=ACT.Ln, bias=sig_shift[:, h, k : k + 1]
+                        out=unit_logs[:, h, :], in_=sig[c][:, h, :], func=ACT.Ln, bias=sig_shift[:, h, k : k + 1]
                     )
-                logs[c * KC + k] = unit_logs
+                logs[j] = unit_logs
 
-        def take_weights(c):
-            for j in range(c * KC, (c + 1) * KC):
-                wgt = big_pool.tile([P, H, CHUNK], F32, name="wgt", tag="big", align_bytes=64)
-                if squarer(j) == "vector":
-                    nc.scalar.activation(out=wgt[:], in_=logs[j][:], func=ACT.Exp, bias=ln_half[:], scale=-2.0)
+        def take_weights(units):
+            for j in units:
+                if is_paired(j):
+                    wgt = small_pool.tile([P, CHUNK], F32, name="small_wgt", tag="small", align_bytes=64)
                 else:
-                    nc.scalar.activation(out=wgt[:], in_=logs[j][:], func=ACT.Exp, bias=half_ln_half[:], scale=-1.0)
+                    wgt = big_pool.tile([P, H, CHUNK], F32, name="wgt", tag="big", align_bytes=64)
+                nc.scalar.activation(out=wgt[:], in_=logs[j][:], func=ACT.Exp, bias=half_ln_half[:], scale=-1.0)
                 wgts[j] = wgt
 
         def weighted_squares(j):
             c, k = divmod(j, KC)
             wgt = wgts[j]
-            for step in range(2 if squarer(j) == "vector" else 1):
-                for h in range(H):
-                    nc.vector.scalar_tensor_tensor(
-                        out=wgt[:, h, :],
-                        in0=mu_sums[c][h][:],
-                        scalar=mu_shift[:, h, k : k + 1],
-                        in1=wgt[:, h, :],
-                        op0=ALU.subtract,
-                        op1=ALU.mult,
-                    )
+            for h in range(H):
+                nc.vector.scalar_tensor_tensor(
+                    out=wgt[:, h, :],
+                    in0=mu_sums[c][h][:],
+                    scalar=mu_shift[:, h, k : k + 1],
+                    in1=wgt[:, h, :],
+                    op0=ALU.subtract,
+                    op1=ALU.mult,
+                )
             if squarer(j) == "gpsimd":
                 nc.gpsimd.tensor_tensor(out=wgt[:], in0=wgt[:], in1=wgt[:], op=ALU.mult)
             if squarer(j) == "scalar":
                 nc.scalar.activation(out=wgt[:], in_=wgt[:], func=ACT.Square)
 
         def add_over_halves(j):
-            acc = psum.tile([P, TPC, P], F32, name="acc", tag="acc")
+            acc = acc_psum.tile([P, TPC, P], F32, name="acc", tag="bank")
             for t in range(TPC):
                 cols = slice(t * P, (t + 1) * P)
-                parts = (logs[j][:, 0, cols], logs[j][:, 1, cols], wgts[j][:, 0, cols], wgts[j][:, 1, cols])
+                if is_paired(j):
+                    parts = (logs[j][:, cols], wgts[j][:, 0, cols], wgts[j][:, 1, cols])
+                else:
+                    parts = (logs[j][:, 0, cols], logs[j][:, 1, cols], wgts[j][:, 0, cols], wgts[j][:, 1, cols])
                 for i, part in enumerate(parts):
                     nc.tensor.matmul(
                         out=acc[:, t, :],
@@ -324,52 +408,156 @@ def tile_deepgmm_pa_t_kernel(
                     )
             accs[j] = acc
 
-        def reduce_units(first, end):
-            for j in range(first, end):
-                c, k = divmod(j, KC)
-                nc.vector.tensor_reduce(
-                    out=energy[:, k, c * TPC : (c + 1) * TPC], in_=accs[j][:], axis=AX.X, op=ALU.add
-                )
+        def reduce_unit(j):
+            c, k = divmod(j, KC)
+            nc.vector.tensor_reduce(
+                out=energy[:, k, c * TPC : (c + 1) * TPC], in_=accs[j][:], axis=AX.X, op=ALU.add
+            )
 
-        prepare(0)
+        sig_sums(0)
+        sig_clamp(0)
         softplus_exp(0)
         softplus_log(0)
         nc.scalar.activation(out=ln_half[:], in_=half[:], func=ACT.Ln)
-        prepare(1)
+        nc.scalar.activation(out=half_ln_half[:], in_=ln_half[:], func=ACT.Copy, scale=0.5)
+        regroup_w(0)
+        nc.vector.tensor_scalar(
+            out=sig_shift[:],
+            in0=par[:, :, ROW_PHI_SIGS : ROW_PHI_SIGS + KC],
+            scalar1=SIG_FLOOR,
+            scalar2=None,
+            op0=ALU.add,
+        )
+        sig_sums(0)
+        quantize_w(0)
         softplus_max(0)
-        take_logs(0)
-        for c in range(2, N_CHUNKS):
-            prepare(c)
-        store_enc_sig(0)
-        nc.vector.tensor_scalar(out=half_ln_half[:], in0=ln_half[:], scalar1=0.5, scalar2=None, op0=ALU.mult)
-        mu_sums[0] = d_layout_sums(0, 0)
-        take_weights(0)
-        for c in range(1, N_CHUNKS):
-            softplus_exp(c)
+        for h in range(H):
+            nc.vector.tensor_scalar(
+                out=mu_shift[:, h, :],
+                in0=par[:, h, ROW_PHI_MUS : ROW_PHI_MUS + KC],
+                scalar1=par[:, h, ROW_BE_MU : ROW_BE_MU + 1],
+                scalar2=None,
+                op0=ALU.subtract,
+            )
+        mu_sums[0] = d_layout_sums(0, 0, mu_psum)
+        nc.vector.tensor_copy(out=be_mu_rows[:], in_=be_mu_bf[:])
+        nc.vector.tensor_copy(out=logit_rows[:], in_=logit_bf[:])
+        pair_rows = keep.tile([P, len(PAIRED_FIRST), D], F32, name="pair_rows")
+        nc.vector.tensor_copy(out=pair_rows[:], in_=pair_bf[:])
 
-        reduced = 0
-        for c in range(N_CHUNKS):
-            for j in range(c * KC, (c + 1) * KC):
-                if j == c * KC + NEXT_CHUNK_AT and c + 1 < N_CHUNKS:
-                    if c == 0:
-                        reduce_units(reduced, j)
-                        reduced = j
-                        for b in range(1, N_CHUNKS + 1):
-                            if b < N_CHUNKS:
-                                softplus_log(b)
-                                softplus_max(b)
-                            if b > 1:
-                                store_enc_sig(b - 1)
-                    mu_sums[c + 1] = d_layout_sums(c + 1, 0)
-                    take_logs(c + 1)
+        def transposing(c):
+            return (lambda: transpose_y(c), lambda: regroup_y(c))
+
+        def clamping(c):
+            def first():
+                quantize_y(c)
+                sig_sums(c)
+
+            return (first, lambda: sig_clamp(c))
+
+        def storing_mu(c):
+            return (lambda: mu_rows(c), lambda: store_enc_mu(c))
+
+        def maximum(c):
+            return (lambda: sig_sums(c), lambda: softplus_max(c))
+
+        def storing_sig(c):
+            return (lambda: sig_rows(c), lambda: store_enc_sig(c))
+
+        batches = [range(a, b) for a, b in zip((0,) + ENDS, ENDS)]
+        take_logs(batches[0], False)
+        sig_rows(0)
+        store_enc_sig(0)
+        for j in batches[0]:
+            if is_paired(j):
+                std_banks(j, (1,))
+                multiply_pair(j)
+        take_logs(batches[0], True)
+        for piece in (transposing(1), clamping(1), storing_mu(1), storing_mu(0)):
+            piece[0]()
+            piece[1]()
+
+        pieces = {}
+        at_unit = {}
+        load_at = {}
+        def at(j, f):
+            at_unit.setdefault(j, []).append(f)
+        FIRST_PIECE, EXP_AT, LOG_LAG, PIECE_STEP = PARS
+        for b, batch in enumerate(batches):
+            at(batch.start, lambda b=b: take_weights(batches[b]))
+            if b + 1 < len(batches):
+                nxt = batches[b + 1]
+                new = [c for c in range(1, N_CHUNKS) if batch.stop <= c * KC + (0 if b else 16) and c * KC < nxt.stop and c * KC >= (batch.stop if b else 0)]
+                ns = batch.stop - batch.start
+                t = batch.start
+                def first(new=new):
+                    for c in new:
+                        if c > 1:
+                            transpose_y(c)
+                            regroup_y(c)
+                    for c in new:
+                        if c > 1:
+                            quantize_y(c)
+                            sig_sums(c)
+                            sig_clamp(c)
+                at(batch.start, first)
+                for c in new:
+                    if c > 1:
+                        pieces[t + FIRST_PIECE] = storing_mu(c)
+                        t += PIECE_STEP
+                for c in new:
+                    if c > 1:
+                        load_at.setdefault(max(batch.start - 4, 0), []).append(c)
+                tl = max(batch.start + 1, batch.stop - int(EXP_AT))
+                def nextphase(b=b, new=new):
+                    for c in new:
+                        softplus_exp(c)
+                    for c in new:
+                        softplus_log(c)
+                at(tl, nextphase)
+                t = tl + LOG_LAG
+                for c in new:
+                    pieces[t] = maximum(c)
+                    t += PIECE_STEP
+                def tl2(b=b):
+                    take_logs(batches[b + 1], False)
+                at(t, tl2)
+                for c in new:
+                    pieces[t] = storing_sig(c)
+                    t += PIECE_STEP
+                for j in nxt:
+                    if is_paired(j):
+                        pieces[t] = (lambda j=j: std_banks(j, (1,)), lambda j=j: multiply_pair(j))
+                        t += 1
+                t += 1
+                assert t < nxt.start or not b, (b, t)
+                at(t, lambda b=b: take_logs(batches[b + 1], True))
+
+        for j in range(N_UNITS + REDUCE_LAG):
+            c, k = divmod(j, KC)
+            flushed = (j in at_unit or is_paired(j)) and j - 1 in pieces
+            if flushed:
+                pieces[j - 1][1]()
+            for b in load_at.get(j, ()):
+                load_y(b)
+            if j < N_UNITS:
+                for f in at_unit.get(j, ()):
+                    f()
+                if is_paired(j):
+                    divide_pair(j)
                 weighted_squares(j)
-                add_over_halves(j)
-                if j - REDUCE_LAG >= reduced:
-                    reduce_units(reduced, j - REDUCE_LAG + 1)
-                    reduced = j - REDUCE_LAG + 1
-            if c + 1 < N_CHUNKS:
-                take_weights(c + 1)
-        reduce_units(reduced, N_UNITS)
+                if k == KC - 1 and c + 1 < N_CHUNKS:
+                    mu_sums[c + 1] = d_layout_sums(c + 1, 0, mu_psum)
+            if j - 1 in pieces and not flushed:
+                pieces[j - 1][1]()
+            if j in pieces:
+                pieces[j][0]()
+            if j + 1 < N_UNITS and is_paired(j + 1):
+                std_banks(j + 1, (1, 0))
+            if SUM_LAG <= j < N_UNITS + SUM_LAG:
+                add_over_halves(j - SUM_LAG)
+            if j >= REDUCE_LAG:
+                reduce_unit(j - REDUCE_LAG)
 
         z = keep.tile([P, N_TILES, KC], F32, name="z")
         z_max = keep.tile([P, N_TILES], F32, name="z_max")

@@ -33,19 +33,21 @@ ROW_PHI_SIGS = KC
 ROW_BE_MU = 2 * KC
 ROW_BE_SIG = 2 * KC + 1
 
-ENDS = (16, 38, 60, 82, 104, 120, 128)
-PARS = (1, 10, 1, 1)
-PAIRED = (4, 12)
-PAIRED_FIRST = (4, 8, 12)
-PAIRED_END = 112
-SCALAR_FROM = 0
+ENDS = (16, 40, 62, 86, 106, 120, 128)
+PARS = (0, 11, 1, 2)
+PAIR_FROM = 8
+GROUP = 4
+TAIL_FROM = 120
 SUM_LAG = 3
 REDUCE_LAG = 5
-BIG_SLOTS = 32
-SIG_OUT_SLOTS = 3
-PAIR_SLOTS = 3
-SMALL_SLOTS = 8
+BIG_SLOTS = 37
+SIG_OUT_SLOTS = 2
+SMALL_SLOTS = 4
 STAGE_SLOTS = 3
+
+
+VEC_EVERY = 5
+VEC_AT = 1
 
 FLOPS = 2 * N_ROWS * K_IN * 2 * D
 
@@ -57,7 +59,7 @@ def tile_deepgmm_pa_t_kernel(
     y_view = Y.rearrange("(p t) k -> p (t k)", t=N_TILES)
     mu_view = out_0.rearrange("(p t) d -> p t d", t=N_TILES)
     sig_view = out_1.rearrange("(p t) d -> p t d", t=N_TILES)
-    z_view = out_2.rearrange("(p t) k -> p (t k)", t=N_TILES)
+    z_view = out_2.rearrange("(p t) k -> p t k", t=N_TILES)
 
     with ExitStack() as ctx:
         ctx.enter_context(tc.manual_schedule())
@@ -75,6 +77,12 @@ def tile_deepgmm_pa_t_kernel(
         half = keep.tile([P, 1], F32, name="half")
         ln_half = keep.tile([P, 1], F32, name="ln_half")
         half_ln_half = keep.tile([P, 1], F32, name="half_ln_half")
+        early_tiles = slice(0, N_TILES - TPC)
+        last_tiles = slice(N_TILES - TPC, N_TILES)
+        z = keep.tile([P, N_TILES, KC], F32, name="z")
+        z_max = keep.tile([P, N_TILES], F32, name="z_max")
+        z_exp = keep.tile([P, N_TILES, KC], F32, name="z_exp")
+        z_sum = keep.tile([P, N_TILES], F32, name="z_sum")
         energy = keep.tile([P, KC, N_TILES], F32, name="energy")
 
         big_pool = ctx.enter_context(tc.tile_pool(name="big", bufs=BIG_SLOTS))
@@ -86,7 +94,6 @@ def tile_deepgmm_pa_t_kernel(
         acc_psum = ctx.enter_context(tc.psum_pool(name="acc_psum", bufs=3))
 
         sig_out_pool = ctx.enter_context(tc.tile_pool(name="sig_outs", bufs=SIG_OUT_SLOTS))
-        pair_pool = ctx.enter_context(tc.tile_pool(name="pairs", bufs=PAIR_SLOTS))
         small_pool = ctx.enter_context(tc.tile_pool(name="smalls", bufs=SMALL_SLOTS))
         sig_outs = {}
         codes = {}
@@ -172,10 +179,6 @@ def tile_deepgmm_pa_t_kernel(
         nc.sync.dma_start(out=be_mu_bf[:], in_=be_mu.partition_broadcast(P))
         logit_bf = keep.tile([P, KC], BF16, name="logit_bf")
         nc.sync.dma_start(out=logit_bf[:], in_=phi_logits.partition_broadcast(P))
-        pair_bf = keep.tile([P, len(PAIRED_FIRST), D], BF16, name="pair_bf")
-        for i, k in enumerate(PAIRED_FIRST):
-            nc.sync.dma_start(out=pair_bf[:, i, :], in_=phi_sigs[k, :].partition_broadcast(P))
-
         w_grps = {}
 
         def regroup_w(m):
@@ -294,59 +297,56 @@ def tile_deepgmm_pa_t_kernel(
         mu_sums = {}
 
         def squarer(j):
-            if j >= N_UNITS - KC + SCALAR_FROM and j % 2 == 1:
+            if j >= TAIL_FROM:
                 return "scalar"
+            if j % VEC_EVERY == VEC_AT and not is_paired(j):
+                return "vector"
             return "gpsimd"
 
         def is_paired(j):
-            return j % KC in (PAIRED_FIRST if j < KC else PAIRED) and j < PAIRED_END and j not in ENDS
+            return PAIR_FROM <= j < ENDS[0]
 
-        stds = {}
+        def starts_pair(j):
+            return is_paired(j) and (j - PAIR_FROM) % GROUP == 0
 
-        def std_banks(j, halves):
-            c, k = divmod(j, KC)
-            stds[j] = {}
-            for h in halves:
-                std = stage_psum.tile([P, TPC, P], F32, name="std", tag="bank")
+        sig_back = {}
+
+        def sig_banks(c):
+            sig_back[c] = []
+            for h in range(H):
+                bank = stage_psum.tile([P, TPC, P], F32, name="sig_back", tag="bank")
                 for t in range(TPC):
-                    parts = (
-                        sig_outs[c][:, t, h * P : (h + 1) * P],
-                        pair_rows[:, PAIRED_FIRST.index(k), h * P : (h + 1) * P],
-                    )
-                    for i, part in enumerate(parts):
-                        nc.tensor.matmul(
-                            out=std[:, t, :],
-                            lhsT=part,
-                            rhs=ident[:],
-                            is_transpose=True,
-                            start=(i == 0),
-                            stop=(i == len(parts) - 1),
-                        )
-                stds[j][h] = std
+                    nc.tensor.transpose(bank[:, t, :], sig_outs[c][:, t, h * P : (h + 1) * P], ident[:])
+                sig_back[c].append(bank[:].rearrange("p t n -> p (t n)"))
 
-        def multiply_pair(j):
+        def multiply_early(j):
             c, k = divmod(j, KC)
-            product = small_pool.tile([P, CHUNK], F32, name="product", tag="small", align_bytes=64)
+            product = big_pool.tile([P, CHUNK], F32, name="product", tag="big", align_bytes=64)
+            nc.vector.tensor_scalar(
+                out=product[:], in0=sig[c][:, 1, :], scalar1=sig_shift[:, 1, k : k + 1], scalar2=None, op0=ALU.add
+            )
             nc.vector.scalar_tensor_tensor(
                 out=product[:],
                 in0=sig[c][:, 0, :],
                 scalar=sig_shift[:, 0, k : k + 1],
-                in1=stds[j][1][:].rearrange("p t n -> p (t n)"),
+                in1=product[:],
                 op0=ALU.add,
                 op1=ALU.mult,
             )
             logs[j] = product
 
         def divide_pair(j):
-            wgt = pair_pool.tile([P, H, CHUNK], F32, name="pair_wgt")
-            for h in range(H):
-                nc.vector.tensor_tensor(
+            c, k = divmod(j, KC)
+            wgt = wgts[j]
+            for h in (1, 0):
+                nc.vector.scalar_tensor_tensor(
                     out=wgt[:, h, :],
-                    in0=stds[j][1 - h][:].rearrange("p t n -> p (t n)"),
-                    in1=wgts[j][:],
-                    op=ALU.mult,
+                    in0=sig_back[c][1 - h],
+                    scalar=par[:, 1 - h, ROW_PHI_SIGS + k : ROW_PHI_SIGS + k + 1],
+                    in1=wgt[:, 0, :],
+                    op0=ALU.add,
+                    op1=ALU.mult,
                 )
-            wgts[j] = wgt
 
         def take_logs(units, paired):
             for j in units:
@@ -365,35 +365,48 @@ def tile_deepgmm_pa_t_kernel(
 
         def take_weights(units):
             for j in units:
-                if is_paired(j):
-                    wgt = small_pool.tile([P, CHUNK], F32, name="small_wgt", tag="small", align_bytes=64)
-                else:
-                    wgt = big_pool.tile([P, H, CHUNK], F32, name="wgt", tag="big", align_bytes=64)
-                nc.scalar.activation(out=wgt[:], in_=logs[j][:], func=ACT.Exp, bias=half_ln_half[:], scale=-1.0)
+                wgt = big_pool.tile([P, H, CHUNK], F32, name="wgt", tag="big", align_bytes=64)
+                twice = squarer(j) == "vector"
+                nc.scalar.activation(
+                    out=wgt[:, 0, :] if is_paired(j) else wgt[:],
+                    in_=logs[j][:],
+                    func=ACT.Exp,
+                    bias=ln_half[:] if twice else half_ln_half[:],
+                    scale=-2.0 if twice else -1.0,
+                )
                 wgts[j] = wgt
 
         def weighted_squares(j):
             c, k = divmod(j, KC)
             wgt = wgts[j]
-            for h in range(H):
-                nc.vector.scalar_tensor_tensor(
-                    out=wgt[:, h, :],
-                    in0=mu_sums[c][h][:],
-                    scalar=mu_shift[:, h, k : k + 1],
-                    in1=wgt[:, h, :],
-                    op0=ALU.subtract,
-                    op1=ALU.mult,
-                )
+            for step in range(2 if squarer(j) == "vector" else 1):
+                for h in range(H):
+                    nc.vector.scalar_tensor_tensor(
+                        out=wgt[:, h, :],
+                        in0=mu_sums[c][h][:],
+                        scalar=mu_shift[:, h, k : k + 1],
+                        in1=wgt[:, h, :],
+                        op0=ALU.subtract,
+                        op1=ALU.mult,
+                    )
             if squarer(j) == "gpsimd":
                 nc.gpsimd.tensor_tensor(out=wgt[:], in0=wgt[:], in1=wgt[:], op=ALU.mult)
             if squarer(j) == "scalar":
                 nc.scalar.activation(out=wgt[:], in_=wgt[:], func=ACT.Square)
 
+        def gpsimd_adds(j):
+            return j >= TAIL_FROM
+
+        def add_logs(j):
+            log_sum = big_pool.tile([P, CHUNK], F32, name="log_sum", tag="big", align_bytes=64)
+            nc.gpsimd.tensor_tensor(out=log_sum[:], in0=logs[j][:, 0, :], in1=logs[j][:, 1, :], op=ALU.add)
+            logs[j] = log_sum
+
         def add_over_halves(j):
             acc = acc_psum.tile([P, TPC, P], F32, name="acc", tag="bank")
             for t in range(TPC):
                 cols = slice(t * P, (t + 1) * P)
-                if is_paired(j):
+                if is_paired(j) or gpsimd_adds(j):
                     parts = (logs[j][:, cols], wgts[j][:, 0, cols], wgts[j][:, 1, cols])
                 else:
                     parts = (logs[j][:, 0, cols], logs[j][:, 1, cols], wgts[j][:, 0, cols], wgts[j][:, 1, cols])
@@ -413,6 +426,39 @@ def tile_deepgmm_pa_t_kernel(
             nc.vector.tensor_reduce(
                 out=energy[:, k, c * TPC : (c + 1) * TPC], in_=accs[j][:], axis=AX.X, op=ALU.add
             )
+
+        def softmax_shift(tiles):
+            n = tiles.stop - tiles.start
+            nc.vector.tensor_tensor(
+                out=z[:, tiles, :],
+                in0=logit_rows[:].unsqueeze(1).to_broadcast([P, n, KC]),
+                in1=energy[:, :, tiles].rearrange("p k t -> p t k"),
+                op=ALU.subtract,
+            )
+            nc.vector.tensor_reduce(out=z_max[:, tiles], in_=z[:, tiles, :], axis=AX.X, op=ALU.max)
+            nc.vector.tensor_tensor(
+                out=z[:, tiles, :],
+                in0=z[:, tiles, :],
+                in1=z_max[:, tiles].unsqueeze(2).to_broadcast([P, n, KC]),
+                op=ALU.subtract,
+            )
+
+        def softmax_exp(tiles):
+            nc.scalar.activation(out=z_exp[:, tiles, :], in_=z[:, tiles, :], func=ACT.Exp)
+
+        def softmax_sum(tiles):
+            nc.vector.tensor_reduce(out=z_sum[:, tiles], in_=z_exp[:, tiles, :], axis=AX.X, op=ALU.add)
+            nc.scalar.activation(out=z_sum[:, tiles], in_=z_sum[:, tiles], func=ACT.Ln)
+
+        def softmax_end(tiles):
+            n = tiles.stop - tiles.start
+            nc.vector.tensor_tensor(
+                out=z[:, tiles, :],
+                in0=z[:, tiles, :],
+                in1=z_sum[:, tiles].unsqueeze(2).to_broadcast([P, n, KC]),
+                op=ALU.subtract,
+            )
+            nc.sync.dma_start(out=z_view[:, tiles, :], in_=z[:, tiles, :])
 
         sig_sums(0)
         sig_clamp(0)
@@ -442,8 +488,6 @@ def tile_deepgmm_pa_t_kernel(
         mu_sums[0] = d_layout_sums(0, 0, mu_psum)
         nc.vector.tensor_copy(out=be_mu_rows[:], in_=be_mu_bf[:])
         nc.vector.tensor_copy(out=logit_rows[:], in_=logit_bf[:])
-        pair_rows = keep.tile([P, len(PAIRED_FIRST), D], F32, name="pair_rows")
-        nc.vector.tensor_copy(out=pair_rows[:], in_=pair_bf[:])
 
         def transposing(c):
             return (lambda: transpose_y(c), lambda: regroup_y(c))
@@ -465,14 +509,13 @@ def tile_deepgmm_pa_t_kernel(
             return (lambda: sig_rows(c), lambda: store_enc_sig(c))
 
         batches = [range(a, b) for a, b in zip((0,) + ENDS, ENDS)]
-        take_logs(batches[0], False)
-        sig_rows(0)
-        store_enc_sig(0)
         for j in batches[0]:
             if is_paired(j):
-                std_banks(j, (1,))
-                multiply_pair(j)
+                multiply_early(j)
+        take_logs(batches[0], False)
         take_logs(batches[0], True)
+        sig_rows(0)
+        store_enc_sig(0)
         for piece in (transposing(1), clamping(1), storing_mu(1), storing_mu(0)):
             piece[0]()
             piece[1]()
@@ -487,28 +530,18 @@ def tile_deepgmm_pa_t_kernel(
             at(batch.start, lambda b=b: take_weights(batches[b]))
             if b + 1 < len(batches):
                 nxt = batches[b + 1]
-                new = [c for c in range(1, N_CHUNKS) if batch.stop <= c * KC + (0 if b else 16) and c * KC < nxt.stop and c * KC >= (batch.stop if b else 0)]
-                ns = batch.stop - batch.start
-                t = batch.start
-                def first(new=new):
-                    for c in new:
-                        if c > 1:
-                            transpose_y(c)
-                            regroup_y(c)
-                    for c in new:
-                        if c > 1:
-                            quantize_y(c)
-                            sig_sums(c)
-                            sig_clamp(c)
-                at(batch.start, first)
-                for c in new:
-                    if c > 1:
-                        pieces[t + FIRST_PIECE] = storing_mu(c)
-                        t += PIECE_STEP
-                for c in new:
-                    if c > 1:
-                        load_at.setdefault(max(batch.start - 4, 0), []).append(c)
-                tl = max(batch.start + 1, batch.stop - int(EXP_AT))
+                new = [c for c in range(1, N_CHUNKS) if nxt.start <= c * KC < nxt.stop]
+                later = [c for c in new if c > 1]
+                t = max(batch.start - len(later) - 1 + FIRST_PIECE, 0)
+                for c in later:
+                    load_at.setdefault(max(t - 4, 0), []).append(c)
+                for kind in (transposing, clamping, storing_mu):
+                    for c in later:
+                        if t == batch.start:
+                            t += 1
+                        pieces[t] = kind(c)
+                        t += 1 if kind is transposing else PIECE_STEP
+                tl = max(t, batch.start + 1, batch.stop - EXP_AT)
                 def nextphase(b=b, new=new):
                     for c in new:
                         softplus_exp(c)
@@ -525,17 +558,10 @@ def tile_deepgmm_pa_t_kernel(
                 for c in new:
                     pieces[t] = storing_sig(c)
                     t += PIECE_STEP
-                for j in nxt:
-                    if is_paired(j):
-                        pieces[t] = (lambda j=j: std_banks(j, (1,)), lambda j=j: multiply_pair(j))
-                        t += 1
-                t += 1
-                assert t < nxt.start or not b, (b, t)
-                at(t, lambda b=b: take_logs(batches[b + 1], True))
 
         for j in range(N_UNITS + REDUCE_LAG):
             c, k = divmod(j, KC)
-            flushed = (j in at_unit or is_paired(j)) and j - 1 in pieces
+            flushed = (j in at_unit or starts_pair(j)) and j - 1 in pieces
             if flushed:
                 pieces[j - 1][1]()
             for b in load_at.get(j, ()):
@@ -543,40 +569,33 @@ def tile_deepgmm_pa_t_kernel(
             if j < N_UNITS:
                 for f in at_unit.get(j, ()):
                     f()
-                if is_paired(j):
-                    divide_pair(j)
+                if starts_pair(j):
+                    if j in at_unit:
+                        sig_banks(c)
+                    for i in range(j, j + GROUP):
+                        divide_pair(i)
                 weighted_squares(j)
+                if gpsimd_adds(j):
+                    add_logs(j)
                 if k == KC - 1 and c + 1 < N_CHUNKS:
                     mu_sums[c + 1] = d_layout_sums(c + 1, 0, mu_psum)
             if j - 1 in pieces and not flushed:
                 pieces[j - 1][1]()
             if j in pieces:
                 pieces[j][0]()
-            if j + 1 < N_UNITS and is_paired(j + 1):
-                std_banks(j + 1, (1, 0))
+            if starts_pair(j + 1) and j + 1 not in at_unit:
+                sig_banks((j + 1) // KC)
             if SUM_LAG <= j < N_UNITS + SUM_LAG:
                 add_over_halves(j - SUM_LAG)
             if j >= REDUCE_LAG:
                 reduce_unit(j - REDUCE_LAG)
-
-        z = keep.tile([P, N_TILES, KC], F32, name="z")
-        z_max = keep.tile([P, N_TILES], F32, name="z_max")
-        z_exp = keep.tile([P, N_TILES, KC], F32, name="z_exp")
-        z_sum = keep.tile([P, N_TILES], F32, name="z_sum")
-        nc.vector.tensor_tensor(
-            out=z[:],
-            in0=logit_rows[:].unsqueeze(1).to_broadcast([P, N_TILES, KC]),
-            in1=energy[:].rearrange("p k t -> p t k"),
-            op=ALU.subtract,
-        )
-        nc.vector.tensor_reduce(out=z_max[:], in_=z[:], axis=AX.X, op=ALU.max)
-        nc.vector.tensor_tensor(
-            out=z[:], in0=z[:], in1=z_max[:].unsqueeze(2).to_broadcast([P, N_TILES, KC]), op=ALU.subtract
-        )
-        nc.scalar.activation(out=z_exp[:], in_=z[:], func=ACT.Exp)
-        nc.vector.tensor_reduce(out=z_sum[:], in_=z_exp[:], axis=AX.X, op=ALU.add)
-        nc.scalar.activation(out=z_sum[:], in_=z_sum[:], func=ACT.Ln)
-        nc.vector.tensor_tensor(
-            out=z[:], in0=z[:], in1=z_sum[:].unsqueeze(2).to_broadcast([P, N_TILES, KC]), op=ALU.subtract
-        )
-        nc.sync.dma_start(out=z_view, in_=z[:].rearrange("p t k -> p (t k)"))
+            if j - REDUCE_LAG == N_UNITS - KC - 1:
+                softmax_shift(early_tiles)
+            if j == N_UNITS - 2:
+                softmax_exp(early_tiles)
+            if j == N_UNITS:
+                softmax_sum(early_tiles)
+            if j == N_UNITS + 2:
+                softmax_end(early_tiles)
+        for step in (softmax_shift, softmax_exp, softmax_sum, softmax_end):
+            step(last_tiles)

@@ -33,14 +33,14 @@ ROW_PHI_SIGS = KC
 ROW_BE_MU = 2 * KC
 ROW_BE_SIG = 2 * KC + 1
 
-ENDS = (16, 40, 62, 86, 106, 120, 128)
-PARS = (0, 11, 1, 2)
+ENDS = (16, 36, 60, 84, 104, 118, 128)
+PARS = (0, 11, 0, 2)
 PAIR_FROM = 8
 GROUP = 4
 TAIL_FROM = 120
 SUM_LAG = 3
 REDUCE_LAG = 5
-BIG_SLOTS = 37
+BIG_SLOTS = 41
 SIG_OUT_SLOTS = 2
 SMALL_SLOTS = 4
 STAGE_SLOTS = 3
@@ -448,10 +448,10 @@ def tile_deepgmm_pa_t_kernel(
 
         def softmax_sum(tiles):
             nc.vector.tensor_reduce(out=z_sum[:, tiles], in_=z_exp[:, tiles, :], axis=AX.X, op=ALU.add)
-            nc.scalar.activation(out=z_sum[:, tiles], in_=z_sum[:, tiles], func=ACT.Ln)
 
         def softmax_end(tiles):
             n = tiles.stop - tiles.start
+            nc.scalar.activation(out=z_sum[:, tiles], in_=z_sum[:, tiles], func=ACT.Ln)
             nc.vector.tensor_tensor(
                 out=z[:, tiles, :],
                 in0=z[:, tiles, :],
@@ -591,11 +591,11 @@ def tile_deepgmm_pa_t_kernel(
                 reduce_unit(j - REDUCE_LAG)
             if j - REDUCE_LAG == N_UNITS - KC - 1:
                 softmax_shift(early_tiles)
-            if j == N_UNITS - 2:
-                softmax_exp(early_tiles)
             if j == N_UNITS:
-                softmax_sum(early_tiles)
+                softmax_exp(early_tiles)
             if j == N_UNITS + 2:
-                softmax_end(early_tiles)
-        for step in (softmax_shift, softmax_exp, softmax_sum, softmax_end):
-            step(last_tiles)
+                softmax_sum(early_tiles)
+        softmax_shift(last_tiles)
+        softmax_exp(last_tiles)
+        softmax_sum(last_tiles)
+        softmax_end(slice(0, N_TILES))

from contextlib import ExitStack

import concourse.mybir as mybir
from concourse.masks import make_identity

F32 = mybir.dt.float32
BF16 = mybir.dt.bfloat16
U32 = mybir.dt.uint32
U8 = mybir.dt.uint8
FP8X4 = mybir.dt.float8_e4m3fn_x4
ALU = mybir.AluOpType
ACT = mybir.ActivationFunctionType
AX = mybir.AxisListType

P = 128
N_ROWS = 4096
K_IN = 512
D = 256
H = D // P
KC = 16
CHUNK = 512
TPC = CHUNK // P
N_CHUNKS = N_ROWS // CHUNK
N_TILES = N_ROWS // P
N_UNITS = N_CHUNKS * KC
PACK = 4

SIG_FLOOR = 0.001
SOFTPLUS_LINEAR_FROM = 40.0

ROW_PHI_MUS = 0
ROW_PHI_SIGS = KC
ROW_BE_MU = 2 * KC
ROW_BE_SIG = 2 * KC + 1

ENDS = (16, 36, 60, 84, 104, 118, 128)
PARS = (0, 11, 0, 2)
PAIR_FROM = 8
GROUP = 4
TAIL_FROM = 120
SUM_LAG = 3
REDUCE_LAG = 5
BIG_SLOTS = 41
SIG_OUT_SLOTS = 2
SMALL_SLOTS = 4
STAGE_SLOTS = 3


VEC_EVERY = 5
VEC_AT = 1

FLOPS = 2 * N_ROWS * K_IN * 2 * D


def tile_deepgmm_pa_t_kernel(
    tc, Y, We_mu, be_mu, We_sig, be_sig, phi_mus, phi_sigs, phi_logits, out_0, out_1, out_2
):
    nc = tc.nc
    y_view = Y.rearrange("(p t) k -> p (t k)", t=N_TILES)
    mu_view = out_0.rearrange("(p t) d -> p t d", t=N_TILES)
    sig_view = out_1.rearrange("(p t) d -> p t d", t=N_TILES)
    z_view = out_2.rearrange("(p t) k -> p t k", t=N_TILES)

    with ExitStack() as ctx:
        ctx.enter_context(tc.manual_schedule())
        keep = ctx.enter_context(tc.tile_pool(name="keep", bufs=1))

        ident = keep.tile([P, P], F32, name="ident")
        w_codes = keep.tile([P, 2 * D], U32, name="w_codes", align_bytes=64)
        w_scales = keep.tile([P, 2 * D], U8, name="w_scales", align_bytes=64)
        par = keep.tile([P, H, P], F32, name="par")
        mu_shift = keep.tile([P, H, KC], F32, name="mu_shift")
        sig_shift = keep.tile([P, H, KC], F32, name="sig_shift")
        be_mu_rows = keep.tile([P, D], F32, name="be_mu_rows")
        logit_rows = keep.tile([P, KC], F32, name="logit_rows")
        one = keep.tile([P, 1], F32, name="one")
        half = keep.tile([P, 1], F32, name="half")
        ln_half = keep.tile([P, 1], F32, name="ln_half")
        half_ln_half = keep.tile([P, 1], F32, name="half_ln_half")
        early_tiles = slice(0, N_TILES - TPC)
        last_tiles = slice(N_TILES - TPC, N_TILES)
        z = keep.tile([P, N_TILES, KC], F32, name="z")
        z_max = keep.tile([P, N_TILES], F32, name="z_max")
        z_exp = keep.tile([P, N_TILES, KC], F32, name="z_exp")
        z_sum = keep.tile([P, N_TILES], F32, name="z_sum")
        energy = keep.tile([P, KC, N_TILES], F32, name="energy")

        big_pool = ctx.enter_context(tc.tile_pool(name="big", bufs=BIG_SLOTS))
        y_pool = ctx.enter_context(tc.tile_pool(name="ys", bufs=3))
        stage_pool = ctx.enter_context(tc.tile_pool(name="stages", bufs=STAGE_SLOTS))
        out_pool = ctx.enter_context(tc.tile_pool(name="outs", bufs=2))
        mu_psum = ctx.enter_context(tc.psum_pool(name="mu_psum", bufs=3))
        stage_psum = ctx.enter_context(tc.psum_pool(name="stage_psum", bufs=2))
        acc_psum = ctx.enter_context(tc.psum_pool(name="acc_psum", bufs=3))

        sig_out_pool = ctx.enter_context(tc.tile_pool(name="sig_outs", bufs=SIG_OUT_SLOTS))
        small_pool = ctx.enter_context(tc.tile_pool(name="smalls", bufs=SMALL_SLOTS))
        sig_outs = {}
        codes = {}
        scales = {}
        sig = {}

        def d_layout_sums(c, first_block, pool):
            sums = []
            for h in range(H):
                cols = slice((first_block + h) * P, (first_block + h + 1) * P)
                d_sum = pool.tile([P, CHUNK], F32, name="d_sum", tag="bank")
                nc.tensor.matmul_mx(
                    out=d_sum[:],
                    lhsT=w_codes[:, cols].bitcast(FP8X4),
                    lhsT_scale=w_scales[:, cols],
                    rhs=codes[c][:].bitcast(FP8X4),
                    rhs_scale=scales[c][:],
                    start=True,
                    stop=True,
                )
                sums.append(d_sum)
            return sums

        make_identity(nc, ident[:])

        rows_bf = keep.tile([P, D], BF16, name="rows_bf")
        nc.vector.memset(rows_bf[:], 0.0)
        nc.vector.memset(one[:], 1.0)
        nc.vector.memset(half[:], 0.5)
        nc.scalar.dma_start(out=rows_bf[ROW_PHI_MUS : ROW_PHI_MUS + KC, :], in_=phi_mus)
        nc.scalar.dma_start(out=rows_bf[ROW_PHI_SIGS : ROW_PHI_SIGS + KC, :], in_=phi_sigs)
        nc.scalar.dma_start(out=rows_bf[ROW_BE_MU : ROW_BE_MU + 1, :], in_=be_mu.rearrange("(o d) -> o d", o=1))
        nc.scalar.dma_start(out=rows_bf[ROW_BE_SIG : ROW_BE_SIG + 1, :], in_=be_sig.rearrange("(o d) -> o d", o=1))
        nc.scalar.activation(out=ln_half[:], in_=half[:], func=ACT.Exp)

        y_raw = {}
        y_banks = {}
        y_grps = {}

        def load_y(c):
            y_chunk = y_pool.tile([P, TPC * K_IN], BF16, name="y_chunk", tag="y", align_bytes=64)
            nc.sync.dma_start(out=y_chunk[:], in_=y_view[:, c * TPC * K_IN : (c + 1) * TPC * K_IN])
            y_raw[c] = y_chunk

        def transpose_y(c):
            words = y_raw[c][:].bitcast(F32)
            y_banks[c] = []
            for pair in range(TPC // 2):
                y_t = stage_psum.tile([P, 2, 2 * P], F32, name="y_t", tag="bank")
                for i in range(2):
                    first_word = (2 * pair + i) * (K_IN // 2)
                    for u in range(2):
                        nc.tensor.transpose(
                            y_t[:, u, i * P : (i + 1) * P],
                            words[:, first_word + u : first_word + K_IN // 2 : 2],
                            ident[:],
                        )
                y_banks[c].append(y_t)

        def regroup_y(c):
            y_grp = y_pool.tile([P, PACK * CHUNK], BF16, name="y_grp", tag="y", align_bytes=64)
            grp_words = y_grp[:].bitcast(F32)
            for pair in range(TPC // 2):
                copy = nc.scalar.copy if c == 0 and pair == 1 else nc.vector.tensor_copy
                copy(
                    out=grp_words[:, pair * 4 * P : (pair + 1) * 4 * P].rearrange("p (n u) -> p n u", u=2),
                    in_=y_banks[c][pair][:].rearrange("p u n -> p n u"),
                )
            y_grps[c] = y_grp

        def quantize_y(c):
            codes[c] = stage_pool.tile([P, CHUNK], U32, name="y_codes", align_bytes=64)
            scales[c] = stage_pool.tile([P, CHUNK], U8, name="y_scales", align_bytes=64)
            nc.vector.quantize_mx(out=codes[c][:].bitcast(FP8X4), scales=scales[c][:], in_=y_grps[c][:])

        load_y(0)
        w_raw = {}
        for m, weight in ((1, We_sig), (0, We_mu)):
            w_raw[m] = small_pool.tile([P, PACK, D], BF16, name="w_raw", tag="small", align_bytes=64)
            nc.sync.dma_start(out=w_raw[m][:], in_=weight.rearrange("(q t) c -> q t c", t=PACK))
        load_y(1)
        be_mu_bf = keep.tile([P, D], BF16, name="be_mu_bf")
        nc.sync.dma_start(out=be_mu_bf[:], in_=be_mu.partition_broadcast(P))
        logit_bf = keep.tile([P, KC], BF16, name="logit_bf")
        nc.sync.dma_start(out=logit_bf[:], in_=phi_logits.partition_broadcast(P))
        w_grps = {}

        def regroup_w(m):
            w_grps[m] = small_pool.tile([P, D, PACK], BF16, name="w_grp", tag="small", align_bytes=64)
            nc.vector.tensor_copy(out=w_grps[m][:], in_=w_raw[m][:].rearrange("p t c -> p c t"))

        def quantize_w(m):
            nc.vector.quantize_mx(
                out=w_codes[:, m * D : (m + 1) * D].bitcast(FP8X4),
                scales=w_scales[:, m * D : (m + 1) * D],
                in_=w_grps[m][:].rearrange("p c t -> p (c t)"),
            )

        transpose_y(0)
        regroup_y(0)
        regroup_w(1)
        rows_f32 = keep.tile([P, D], F32, name="rows_f32")
        nc.vector.tensor_copy(out=rows_f32[:], in_=rows_bf[:])
        quantize_w(1)
        par_ps = stage_psum.tile([P, H, P], F32, name="par_ps", tag="bank")
        for h in range(H):
            nc.tensor.transpose(par_ps[:, h, :], rows_f32[:, h * P : (h + 1) * P], ident[:])
        quantize_y(0)
        nc.vector.tensor_copy(out=par[:], in_=par_ps[:])

        banks = {}

        def sig_sums(c):
            banks[c] = d_layout_sums(c, H, stage_psum)

        def sig_clamp(c):
            sig[c] = stage_pool.tile([P, H, CHUNK], F32, name="sig_t")
            for h in range(H):
                nc.vector.tensor_scalar(
                    out=sig[c][:, h, :],
                    in0=banks[c][h][:],
                    scalar1=par[:, h, ROW_BE_SIG : ROW_BE_SIG + 1],
                    scalar2=SOFTPLUS_LINEAR_FROM,
                    op0=ALU.add,
                    op1=ALU.min,
                )

        def mu_rows(c):
            banks[c] = []
            for pair in range(TPC // 2):
                mu_n = stage_psum.tile([P, 2, D], F32, name="mu_n", tag="bank")
                for i in range(2):
                    cols = slice((2 * pair + i) * P, (2 * pair + i + 1) * P)
                    nc.tensor.matmul_mx(
                        out=mu_n[:, i, :],
                        lhsT=codes[c][:, cols].bitcast(FP8X4),
                        lhsT_scale=scales[c][:, cols],
                        rhs=w_codes[:, 0:D].bitcast(FP8X4),
                        rhs_scale=w_scales[:, 0:D],
                        start=True,
                        stop=True,
                    )
                banks[c].append(mu_n)

        def store_enc_mu(c):
            mu_out = out_pool.tile([P, TPC, D], F32, name="mu_out", tag="rows_out")
            for pair in range(TPC // 2):
                nc.vector.tensor_tensor(
                    out=mu_out[:, 2 * pair : 2 * pair + 2, :],
                    in0=banks[c][pair][:],
                    in1=be_mu_rows[:].unsqueeze(1).to_broadcast([P, 2, D]),
                    op=ALU.add,
                )
            nc.sync.dma_start(out=mu_view[:, c * TPC : (c + 1) * TPC, :], in_=mu_out[:])

        def softplus_exp(c):
            for h in range(H):
                nc.scalar.activation(out=sig[c][:, h, :], in_=sig[c][:, h, :], func=ACT.Exp)

        def softplus_log(c):
            for h in range(H):
                nc.scalar.activation(out=sig[c][:, h, :], in_=sig[c][:, h, :], func=ACT.Ln, bias=one[:])

        def softplus_max(c):
            for h in range(H):
                nc.vector.scalar_tensor_tensor(
                    out=sig[c][:, h, :],
                    in0=banks[c][h][:],
                    scalar=par[:, h, ROW_BE_SIG : ROW_BE_SIG + 1],
                    in1=sig[c][:, h, :],
                    op0=ALU.add,
                    op1=ALU.max,
                )

        def sig_rows(c):
            banks[c] = []
            for pair in range(TPC // 2):
                sig_n = stage_psum.tile([P, 2, D], F32, name="sig_n", tag="bank")
                for i in range(2):
                    cols = slice((2 * pair + i) * P, (2 * pair + i + 1) * P)
                    for h in range(H):
                        nc.tensor.transpose(sig_n[:, i, h * P : (h + 1) * P], sig[c][:, h, cols], ident[:])
                banks[c].append(sig_n)

        def store_enc_sig(c):
            sig_out = sig_out_pool.tile([P, TPC, D], F32, name="sig_out")
            sig_outs[c] = sig_out
            for pair in range(TPC // 2):
                nc.vector.tensor_scalar(
                    out=sig_out[:, 2 * pair : 2 * pair + 2, :],
                    in0=banks[c][pair][:],
                    scalar1=SIG_FLOOR,
                    scalar2=None,
                    op0=ALU.add,
                )
            nc.sync.dma_start(out=sig_view[:, c * TPC : (c + 1) * TPC, :], in_=sig_out[:])

        logs = {}
        wgts = {}
        accs = {}
        mu_sums = {}

        def squarer(j):
            if j >= TAIL_FROM:
                return "scalar"
            if j % VEC_EVERY == VEC_AT and not is_paired(j):
                return "vector"
            return "gpsimd"

        def is_paired(j):
            return PAIR_FROM <= j < ENDS[0]

        def starts_pair(j):
            return is_paired(j) and (j - PAIR_FROM) % GROUP == 0

        sig_back = {}

        def sig_banks(c):
            sig_back[c] = []
            for h in range(H):
                bank = stage_psum.tile([P, TPC, P], F32, name="sig_back", tag="bank")
                for t in range(TPC):
                    nc.tensor.transpose(bank[:, t, :], sig_outs[c][:, t, h * P : (h + 1) * P], ident[:])
                sig_back[c].append(bank[:].rearrange("p t n -> p (t n)"))

        def multiply_early(j):
            c, k = divmod(j, KC)
            product = big_pool.tile([P, CHUNK], F32, name="product", tag="big", align_bytes=64)
            nc.vector.tensor_scalar(
                out=product[:], in0=sig[c][:, 1, :], scalar1=sig_shift[:, 1, k : k + 1], scalar2=None, op0=ALU.add
            )
            nc.vector.scalar_tensor_tensor(
                out=product[:],
                in0=sig[c][:, 0, :],
                scalar=sig_shift[:, 0, k : k + 1],
                in1=product[:],
                op0=ALU.add,
                op1=ALU.mult,
            )
            logs[j] = product

        def divide_pair(j):
            c, k = divmod(j, KC)
            wgt = wgts[j]
            for h in (1, 0):
                nc.vector.scalar_tensor_tensor(
                    out=wgt[:, h, :],
                    in0=sig_back[c][1 - h],
                    scalar=par[:, 1 - h, ROW_PHI_SIGS + k : ROW_PHI_SIGS + k + 1],
                    in1=wgt[:, 0, :],
                    op0=ALU.add,
                    op1=ALU.mult,
                )

        def take_logs(units, paired):
            for j in units:
                c, k = divmod(j, KC)
                if is_paired(j) != paired:
                    continue
                if paired:
                    nc.scalar.activation(out=logs[j][:], in_=logs[j][:], func=ACT.Ln)
                    continue
                unit_logs = big_pool.tile([P, H, CHUNK], F32, name="unit_logs", tag="big", align_bytes=64)
                for h in range(H):
                    nc.scalar.activation(
                        out=unit_logs[:, h, :], in_=sig[c][:, h, :], func=ACT.Ln, bias=sig_shift[:, h, k : k + 1]
                    )
                logs[j] = unit_logs

        def take_weights(units):
            for j in units:
                wgt = big_pool.tile([P, H, CHUNK], F32, name="wgt", tag="big", align_bytes=64)
                twice = squarer(j) == "vector"
                nc.scalar.activation(
                    out=wgt[:, 0, :] if is_paired(j) else wgt[:],
                    in_=logs[j][:],
                    func=ACT.Exp,
                    bias=ln_half[:] if twice else half_ln_half[:],
                    scale=-2.0 if twice else -1.0,
                )
                wgts[j] = wgt

        def weighted_squares(j):
            c, k = divmod(j, KC)
            wgt = wgts[j]
            for step in range(2 if squarer(j) == "vector" else 1):
                for h in range(H):
                    nc.vector.scalar_tensor_tensor(
                        out=wgt[:, h, :],
                        in0=mu_sums[c][h][:],
                        scalar=mu_shift[:, h, k : k + 1],
                        in1=wgt[:, h, :],
                        op0=ALU.subtract,
                        op1=ALU.mult,
                    )
            if squarer(j) == "gpsimd":
                nc.gpsimd.tensor_tensor(out=wgt[:], in0=wgt[:], in1=wgt[:], op=ALU.mult)
            if squarer(j) == "scalar":
                nc.scalar.activation(out=wgt[:], in_=wgt[:], func=ACT.Square)

        def gpsimd_adds(j):
            return j >= TAIL_FROM

        def add_logs(j):
            log_sum = big_pool.tile([P, CHUNK], F32, name="log_sum", tag="big", align_bytes=64)
            nc.gpsimd.tensor_tensor(out=log_sum[:], in0=logs[j][:, 0, :], in1=logs[j][:, 1, :], op=ALU.add)
            logs[j] = log_sum

        def add_over_halves(j):
            acc = acc_psum.tile([P, TPC, P], F32, name="acc", tag="bank")
            for t in range(TPC):
                cols = slice(t * P, (t + 1) * P)
                if is_paired(j) or gpsimd_adds(j):
                    parts = (logs[j][:, cols], wgts[j][:, 0, cols], wgts[j][:, 1, cols])
                else:
                    parts = (logs[j][:, 0, cols], logs[j][:, 1, cols], wgts[j][:, 0, cols], wgts[j][:, 1, cols])
                for i, part in enumerate(parts):
                    nc.tensor.matmul(
                        out=acc[:, t, :],
                        lhsT=part,
                        rhs=ident[:],
                        is_transpose=True,
                        start=(i == 0),
                        stop=(i == len(parts) - 1),
                    )
            accs[j] = acc

        def reduce_unit(j):
            c, k = divmod(j, KC)
            nc.vector.tensor_reduce(
                out=energy[:, k, c * TPC : (c + 1) * TPC], in_=accs[j][:], axis=AX.X, op=ALU.add
            )

        def softmax_shift(tiles):
            n = tiles.stop - tiles.start
            nc.vector.tensor_tensor(
                out=z[:, tiles, :],
                in0=logit_rows[:].unsqueeze(1).to_broadcast([P, n, KC]),
                in1=energy[:, :, tiles].rearrange("p k t -> p t k"),
                op=ALU.subtract,
            )
            nc.vector.tensor_reduce(out=z_max[:, tiles], in_=z[:, tiles, :], axis=AX.X, op=ALU.max)
            nc.vector.tensor_tensor(
                out=z[:, tiles, :],
                in0=z[:, tiles, :],
                in1=z_max[:, tiles].unsqueeze(2).to_broadcast([P, n, KC]),
                op=ALU.subtract,
            )

        def softmax_exp(tiles):
            nc.scalar.activation(out=z_exp[:, tiles, :], in_=z[:, tiles, :], func=ACT.Exp)

        def softmax_sum(tiles):
            nc.vector.tensor_reduce(out=z_sum[:, tiles], in_=z_exp[:, tiles, :], axis=AX.X, op=ALU.add)

        def softmax_end(tiles):
            n = tiles.stop - tiles.start
            nc.scalar.activation(out=z_sum[:, tiles], in_=z_sum[:, tiles], func=ACT.Ln)
            nc.vector.tensor_tensor(
                out=z[:, tiles, :],
                in0=z[:, tiles, :],
                in1=z_sum[:, tiles].unsqueeze(2).to_broadcast([P, n, KC]),
                op=ALU.subtract,
            )
            nc.sync.dma_start(out=z_view[:, tiles, :], in_=z[:, tiles, :])

        sig_sums(0)
        sig_clamp(0)
        softplus_exp(0)
        softplus_log(0)
        nc.scalar.activation(out=ln_half[:], in_=half[:], func=ACT.Ln)
        nc.scalar.activation(out=half_ln_half[:], in_=ln_half[:], func=ACT.Copy, scale=0.5)
        regroup_w(0)
        nc.vector.tensor_scalar(
            out=sig_shift[:],
            in0=par[:, :, ROW_PHI_SIGS : ROW_PHI_SIGS + KC],
            scalar1=SIG_FLOOR,
            scalar2=None,
            op0=ALU.add,
        )
        sig_sums(0)
        quantize_w(0)
        softplus_max(0)
        for h in range(H):
            nc.vector.tensor_scalar(
                out=mu_shift[:, h, :],
                in0=par[:, h, ROW_PHI_MUS : ROW_PHI_MUS + KC],
                scalar1=par[:, h, ROW_BE_MU : ROW_BE_MU + 1],
                scalar2=None,
                op0=ALU.subtract,
            )
        mu_sums[0] = d_layout_sums(0, 0, mu_psum)
        nc.vector.tensor_copy(out=be_mu_rows[:], in_=be_mu_bf[:])
        nc.vector.tensor_copy(out=logit_rows[:], in_=logit_bf[:])

        def transposing(c):
            return (lambda: transpose_y(c), lambda: regroup_y(c))

        def clamping(c):
            def first():
                quantize_y(c)
                sig_sums(c)

            return (first, lambda: sig_clamp(c))

        def storing_mu(c):
            return (lambda: mu_rows(c), lambda: store_enc_mu(c))

        def maximum(c):
            return (lambda: sig_sums(c), lambda: softplus_max(c))

        def storing_sig(c):
            return (lambda: sig_rows(c), lambda: store_enc_sig(c))

        batches = [range(a, b) for a, b in zip((0,) + ENDS, ENDS)]
        for j in batches[0]:
            if is_paired(j):
                multiply_early(j)
        take_logs(batches[0], False)
        take_logs(batches[0], True)
        sig_rows(0)
        store_enc_sig(0)
        for piece in (transposing(1), clamping(1), storing_mu(1), storing_mu(0)):
            piece[0]()
            piece[1]()

        pieces = {}
        at_unit = {}
        load_at = {}
        def at(j, f):
            at_unit.setdefault(j, []).append(f)
        FIRST_PIECE, EXP_AT, LOG_LAG, PIECE_STEP = PARS
        for b, batch in enumerate(batches):
            at(batch.start, lambda b=b: take_weights(batches[b]))
            if b + 1 < len(batches):
                nxt = batches[b + 1]
                new = [c for c in range(1, N_CHUNKS) if nxt.start <= c * KC < nxt.stop]
                later = [c for c in new if c > 1]
                t = max(batch.start - len(later) - 1 + FIRST_PIECE, 0)
                for c in later:
                    load_at.setdefault(max(t - 4, 0), []).append(c)
                for kind in (transposing, clamping, storing_mu):
                    for c in later:
                        if t == batch.start:
                            t += 1
                        pieces[t] = kind(c)
                        t += 1 if kind is transposing else PIECE_STEP
                tl = max(t, batch.start + 1, batch.stop - EXP_AT)
                def nextphase(b=b, new=new):
                    for c in new:
                        softplus_exp(c)
                    for c in new:
                        softplus_log(c)
                at(tl, nextphase)
                t = tl + LOG_LAG
                for c in new:
                    pieces[t] = maximum(c)
                    t += PIECE_STEP
                def tl2(b=b):
                    take_logs(batches[b + 1], False)
                at(t, tl2)
                for c in new:
                    pieces[t] = storing_sig(c)
                    t += PIECE_STEP

        for j in range(N_UNITS + REDUCE_LAG):
            c, k = divmod(j, KC)
            flushed = (j in at_unit or starts_pair(j)) and j - 1 in pieces
            if flushed:
                pieces[j - 1][1]()
            for b in load_at.get(j, ()):
                load_y(b)
            if j < N_UNITS:
                for f in at_unit.get(j, ()):
                    f()
                if starts_pair(j):
                    if j in at_unit:
                        sig_banks(c)
                    for i in range(j, j + GROUP):
                        divide_pair(i)
                weighted_squares(j)
                if gpsimd_adds(j):
                    add_logs(j)
                if k == KC - 1 and c + 1 < N_CHUNKS:
                    mu_sums[c + 1] = d_layout_sums(c + 1, 0, mu_psum)
            if j - 1 in pieces and not flushed:
                pieces[j - 1][1]()
            if j in pieces:
                pieces[j][0]()
            if starts_pair(j + 1) and j + 1 not in at_unit:
                sig_banks((j + 1) // KC)
            if SUM_LAG <= j < N_UNITS + SUM_LAG:
                add_over_halves(j - SUM_LAG)
            if j >= REDUCE_LAG:
                reduce_unit(j - REDUCE_LAG)
            if j - REDUCE_LAG == N_UNITS - KC - 1:
                softmax_shift(early_tiles)
            if j == N_UNITS:
                softmax_exp(early_tiles)
            if j == N_UNITS + 2:
                softmax_sum(early_tiles)
        softmax_shift(last_tiles)
        softmax_exp(last_tiles)
        softmax_sum(last_tiles)
        softmax_end(slice(0, N_TILES))
